import numpy as np
import ml_dtypes


def mxq(x, axis, fmt="e4m3"):
    dtype, down = {"e4m3": (ml_dtypes.float8_e4m3fn, 7), "e5m2": (ml_dtypes.float8_e5m2, 14)}[fmt]
    v = np.moveaxis(np.asarray(x, np.float32).astype(ml_dtypes.bfloat16).astype(np.float64), axis, -1)
    blocks = v.reshape(v.shape[:-1] + (-1, 32))
    amax = np.abs(blocks).max(-1, keepdims=True)
    byte = np.maximum(np.where(amax > 0, np.frexp(amax)[1] - 1 + 127, 0) - down, 1)
    scale = np.exp2(byte - 127.0)
    codes = (blocks / scale).astype(np.float32).astype(dtype).astype(np.float64)
    return np.moveaxis((codes * scale).reshape(v.shape), -1, axis)


WIDE = False


def mx_kscale(k):
    if not WIDE:
        return np.ones(k)
    levels = np.array([10, -10, 5, -5, 0])
    a = np.random.permutation(np.resize(levels, k // 512 * 4)).reshape(k // 512, 4)
    idx = np.arange(k)
    return np.exp2(a[idx // 512, idx % 128 // 32])


BF16 = ml_dtypes.bfloat16


def bf(x):
    return np.asarray(x, np.float32).astype(BF16)


def f64(x):
    return np.asarray(x).astype(np.float64)


B, S, DM, DS = 4, 4096, 512, 256


def setup_inputs():
    s = mx_kscale(DM)
    return {"hidden_states": bf(np.random.standard_normal((B, S, DM)) * s),
            "positional_encodings": bf(np.random.standard_normal((B, S, DM)) * 8.0 / np.sqrt(S)),
            "W": bf(np.random.standard_normal((DS, DM)) / np.sqrt(DM) / s[None, :]),
            "b": bf(np.random.standard_normal(DS) * 0.1)}


def reference(hidden_states, positional_encodings, W, b):
    S_ = hidden_states.shape[1]
    alpha = np.exp(-np.pi / S_)
    hp = (mxq(f64(hidden_states), 2, "e4m3") @ mxq(f64(W), 1, "e4m3").T) + f64(b)
    t = np.arange(S_, dtype=np.float64)
    w = np.exp((S_ - 1.0 - t) * np.log(alpha))
    g = hp * w[None, :, None]
    return mxq(g, 1, "e4m3").transpose(0, 2, 1) @ mxq(f64(positional_encodings), 1, "e4m3")

@@ -1,0 +1,297 @@
+import math
+from contextlib import ExitStack
+
+import concourse.mybir as mybir
+from concourse.masks import make_identity
+
+FLOPS = 2 * 4 * 4096 * 512 * 256 * 2
+
+BF16 = mybir.dt.bfloat16
+F32 = mybir.dt.float32
+I32 = mybir.dt.int32
+U32 = mybir.dt.uint32
+U8 = mybir.dt.uint8
+FP8X4 = mybir.dt.float8_e4m3fn_x4
+ALU = mybir.AluOpType
+ACT = mybir.ActivationFunctionType
+
+P = 128
+BATCH = 4
+SEQ = 4096
+DM = 512
+DS = 256
+CHUNK = 512
+CPB = SEQ // CHUNK
+NCH = BATCH * CPB
+LOAD_AHEAD = 6
+MS = 256
+
+
+def tile_attractorstate_v2_t_kernel(tc, hidden_states, positional_encodings, W, b, out):
+    nc = tc.nc
+    hs_flat = hidden_states.flatten_outer_dims()
+    pe_flat = positional_encodings.flatten_outer_dims()
+    out_flat = out.flatten_outer_dims()
+
+    with ExitStack() as ctx:
+        ctx.enter_context(tc.manual_schedule())
+        const = ctx.enter_context(tc.tile_pool(name="const", bufs=1))
+        loads = ctx.enter_context(tc.tile_pool(name="loads", bufs=LOAD_AHEAD + 2))
+        work2 = ctx.enter_context(tc.tile_pool(name="work2", bufs=2))
+        work3 = ctx.enter_context(tc.tile_pool(name="work3", bufs=3))
+        psum = ctx.enter_context(tc.psum_pool(name="psum", bufs=2))
+
+        hs_t = {}
+        pe_t = {}
+        xt_t = {}
+        hgrp_t = {}
+        hq_t = {}
+        hp_t = {}
+        gj_t = {}
+        ggrp_t = {}
+        gq_t = {}
+        pgrp_t = {}
+        pq_t = {}
+        acc_t = {}
+
+        def load(k):
+            if k < 0 or k >= NCH:
+                return
+            rows = slice(k * CHUNK, (k + 1) * CHUNK)
+            hs_sb = loads.tile([P, 4 * DM], BF16, name="hs_sb")
+            nc.sync.dma_start(out=hs_sb[:], in_=hs_flat[rows, :].rearrange("(p j) d -> p (j d)", j=4))
+            pe_sb = loads.tile([P, 4 * DM], BF16, name="pe_sb")
+            nc.sync.dma_start(out=pe_sb[:], in_=pe_flat[rows, :].rearrange("(p j) d -> p (j d)", j=4))
+            hs_t[k] = hs_sb
+            pe_t[k] = pe_sb
+
+        w_sb = const.tile([P, 2 * DM], BF16, name="w_sb")
+        nc.sync.dma_start(
+            out=w_sb[:].rearrange("p (h d) -> p h d", h=2),
+            in_=W.rearrange("(h p) d -> p h d", p=P),
+        )
+        for k in range(LOAD_AHEAD):
+            load(k)
+
+        age_i = const.tile([P, 4 * CPB], I32, name="age_i")
+        nc.gpsimd.iota(age_i[:], pattern=[[-CHUNK, CPB], [-1, 4]], base=SEQ - 1, channel_multiplier=-4)
+        ident = const.tile([P, P], F32, name="ident")
+        make_identity(nc, ident[:])
+
+        ones = const.tile([P, P], BF16, name="ones")
+        nc.vector.memset(ones[:], 1.0)
+        brow = const.tile([P, DS], BF16, name="brow")
+        nc.vector.memset(brow[:], 0.0)
+        nc.scalar.dma_start(out=brow[0:1, :], in_=b.unsqueeze(0))
+        age_f = const.tile([P, 4 * CPB], F32, name="age_f")
+        nc.vector.tensor_copy(out=age_f[:], in_=age_i[:])
+        wts = const.tile([P, 4 * CPB], F32, name="wts")
+        nc.scalar.activation(out=wts[:], in_=age_f[:], func=ACT.Exp, scale=-math.pi / SEQ)
+
+        w32 = w_sb[:].bitcast(F32)
+        wt = psum.tile([P, 2, DS], F32, name="wt", tag="xt")
+        for h in range(2):
+            for u in range(2):
+                nc.tensor.transpose(
+                    wt[:, u, h * P : (h + 1) * P],
+                    w32[:, h * 256 + u * P : h * 256 + (u + 1) * P],
+                    ident[:],
+                )
+        wgrp = const.tile([P, 4 * DS], BF16, name="wgrp", align_bytes=64)
+        nc.vector.tensor_copy(
+            out=wgrp[:].bitcast(F32).rearrange("q (s u) -> q s u", u=2),
+            in_=wt[:].rearrange("q u s -> q s u"),
+        )
+        wcodes = const.tile([P, DS], U32, name="wcodes", align_bytes=64)
+        wscales = const.tile([P, DS], U8, name="wscales", align_bytes=64)
+
+        bps = psum.tile([P, DS], F32, name="bps", tag="hp")
+        nc.tensor.matmul(out=bps[:], lhsT=ones[:], rhs=brow[:], start=True, stop=True)
+        b_bc = const.tile([P, DS], F32, name="b_bc")
+        nc.vector.tensor_copy(out=b_bc[:], in_=bps[:])
+        nc.vector.quantize_mx(out=wcodes[:].bitcast(FP8X4), scales=wscales[:], in_=wgrp[:])
+        bw_t = []
+        for c in range(CPB):
+            bw = const.tile([P, 4, DS], F32, name="bw%d" % c)
+            for j in range(4):
+                nc.gpsimd.tensor_scalar(
+                    out=bw[:, j, :],
+                    in0=b_bc[:],
+                    scalar1=wts[:, 4 * c + j : 4 * c + j + 1],
+                    scalar2=0.0,
+                    op0=ALU.mult,
+                    op1=ALU.add,
+                )
+            bw_t.append(bw)
+
+        def ok(k):
+            return 0 <= k < NCH
+
+        def st_T(k):
+            if not ok(k):
+                return
+            hs32 = hs_t[k][:].bitcast(F32)
+            banks = []
+            for a in range(2):
+                xt = psum.tile([P, 2, 2, P], F32, name="xt", tag="xt")
+                for jj in range(2):
+                    j = 2 * a + jj
+                    for u in range(2):
+                        nc.tensor.transpose(
+                            xt[:, jj, u, :],
+                            hs32[:, j * 256 + u * P : j * 256 + (u + 1) * P],
+                            ident[:],
+                        )
+                banks.append(xt)
+            xt_t[k] = banks
+
+        def st_A(k):
+            if not ok(k):
+                return
+            hgrp = work2.tile([P, 4 * CHUNK], BF16, name="hgrp", align_bytes=64)
+            h32 = hgrp[:].bitcast(F32).rearrange("q (a t u) -> q a t u", a=4, u=2)
+            for a in range(2):
+                nc.scalar.copy(
+                    out=h32[:, 2 * a : 2 * a + 2, :, :],
+                    in_=xt_t[k][a][:].rearrange("q a u t -> q a t u"),
+                )
+            hgrp_t[k] = hgrp
+
+        def st_QH(k):
+            if not ok(k):
+                return
+            hcodes = work2.tile([P, CHUNK], U32, name="hcodes", align_bytes=64)
+            hscales = work2.tile([P, CHUNK], U8, name="hscales", align_bytes=64)
+            nc.vector.quantize_mx(out=hcodes[:].bitcast(FP8X4), scales=hscales[:], in_=hgrp_t[k][:])
+            hq_t[k] = (hcodes, hscales)
+
+        def st_M1(k):
+            if not ok(k):
+                return
+            hcodes, hscales = hq_t[k]
+            banks = []
+            for a in range(2):
+                hp = psum.tile([P, 2, DS], F32, name="hp", tag="hp")
+                for jj in range(2):
+                    j = 2 * a + jj
+                    nc.tensor.matmul_mx(
+                        out=hp[:, jj, :],
+                        lhsT=hcodes[:, j * P : (j + 1) * P].bitcast(FP8X4),
+                        lhsT_scale=hscales[:, j * P : (j + 1) * P],
+                        rhs=wcodes[:].bitcast(FP8X4),
+                        rhs_scale=wscales[:],
+                        start=True,
+                        stop=True,
+                    )
+                banks.append(hp)
+            hp_t[k] = banks
+
+        def st_E(k):
+            if not ok(k):
+                return
+            c = k % CPB
+            gj = work2.tile([P, 4, DS], BF16, name="gj")
+            for j in range(4):
+                nc.vector.scalar_tensor_tensor(
+                    out=gj[:, j, :],
+                    in0=hp_t[k][j // 2][:, j % 2, :],
+                    scalar=wts[:, 4 * c + j : 4 * c + j + 1],
+                    in1=bw_t[c][:, j, :],
+                    op0=ALU.mult,
+                    op1=ALU.add,
+                )
+            gj_t[k] = gj
+
+        def st_RG(k):
+            if not ok(k):
+                return
+            ggrp = work2.tile([P, 4 * DS], BF16, name="ggrp", align_bytes=64)
+            nc.scalar.copy(
+                out=ggrp[:].rearrange("p (c i t) -> p c t i", i=4, t=4),
+                in_=gj_t[k][:].rearrange("p t (c i) -> p c t i", i=4),
+            )
+            ggrp_t[k] = ggrp
+
+        def st_QG(k):
+            if not ok(k):
+                return
+            gcodes = work2.tile([P, DS], U32, name="gcodes", align_bytes=64)
+            gscales = work2.tile([P, DS], U8, name="gscales", align_bytes=64)
+            nc.vector.quantize_mx(out=gcodes[:].bitcast(FP8X4), scales=gscales[:], in_=ggrp_t[k][:])
+            gq_t[k] = (gcodes, gscales)
+
+        def st_RPs(k):
+            if not ok(k):
+                return
+            pgrp = work3.tile([P, 4 * DM], BF16, name="pgrp", align_bytes=64)
+            pgrp_t[k] = pgrp
+            nc.scalar.copy(
+                out=pgrp[:].rearrange("p (c i t) -> p c t i", i=4, t=4)[:, 0 : MS // 4],
+                in_=pe_t[k][:].rearrange("p (t c i) -> p c t i", t=4, i=4)[:, 0 : MS // 4],
+            )
+
+        def st_RPv(k):
+            if not ok(k):
+                return
+            nc.vector.tensor_copy(
+                out=pgrp_t[k][:].rearrange("p (c i t) -> p c t i", i=4, t=4)[:, MS // 4 : DM // 4],
+                in_=pe_t[k][:].rearrange("p (t c i) -> p c t i", t=4, i=4)[:, MS // 4 : DM // 4],
+            )
+
+        def st_QP(k):
+            if not ok(k):
+                return
+            pcodes = work3.tile([P, DM], U32, name="pcodes", align_bytes=64)
+            pscales = work3.tile([P, DM], U8, name="pscales", align_bytes=64)
+            nc.vector.quantize_mx(out=pcodes[:].bitcast(FP8X4), scales=pscales[:], in_=pgrp_t[k][:])
+            pq_t[k] = (pcodes, pscales)
+
+        def st_M2(k):
+            if not ok(k):
+                return
+            i = k // CPB
+            c = k % CPB
+            if c == 0:
+                acc0 = psum.tile([P, DM], F32, name="acc0", tag="acc0")
+                acc1 = psum.tile([P, DM], F32, name="acc1", tag="acc1")
+                acc_t[i] = (acc0, acc1)
+            gcodes, gscales = gq_t[k]
+            pcodes, pscales = pq_t[k]
+            for h in range(2):
+                nc.tensor.matmul_mx(
+                    out=acc_t[i][h][:],
+                    lhsT=gcodes[:, h * P : (h + 1) * P].bitcast(FP8X4),
+                    lhsT_scale=gscales[:, h * P : (h + 1) * P],
+                    rhs=pcodes[:].bitcast(FP8X4),
+                    rhs_scale=pscales[:],
+                    start=(c == 0),
+                    stop=(c == CPB - 1),
+                )
+
+        def st_OUT(k):
+            if not ok(k) or k % CPB != CPB - 1:
+                return
+            i = k // CPB
+            for h in range(2):
+                o_sb = work2.tile([P, DM], F32, name="o_sb%d" % h)
+                if h == 0:
+                    nc.vector.tensor_copy(out=o_sb[:], in_=acc_t[i][h][:])
+                else:
+                    nc.scalar.copy(out=o_sb[:], in_=acc_t[i][h][:])
+                r0 = i * DS + h * P
+                nc.sync.dma_start(out=out_flat[r0 : r0 + P, :], in_=o_sb[:])
+
+        for k in range(-2, NCH + 1):
+            load(k + LOAD_AHEAD + 2)
+            st_E(k)
+            st_A(k + 1)
+            st_T(k + 2)
+            st_QG(k - 1)
+            st_M2(k - 1)
+            st_RPs(k + 1)
+            st_QH(k + 1)
+            st_M1(k + 1)
+            st_RPv(k + 1)
+            st_RG(k)
+            st_QP(k)
+            st_OUT(k - 1)

@@ -24,7 +24,11 @@ CHUNK = 512
 CPB = SEQ // CHUNK
 NCH = BATCH * CPB
 LOAD_AHEAD = 6
-MS = 256
+SPLIT_EARLY = (240, 272, 0)
+SPLIT = (192, 176, 144)
+G_FROM = 4
+BW_ON_VECTOR = 4
+PGRP_BUFS = 3
 
 
 def tile_attractorstate_v2_t_kernel(tc, hidden_states, positional_encodings, W, b, out):
@@ -88,6 +92,27 @@ def tile_attractorstate_v2_t_kernel(tc, hidden_states, positional_encodings, W, 
         wts = const.tile([P, 4 * CPB], F32, name="wts")
         nc.scalar.activation(out=wts[:], in_=age_f[:], func=ACT.Exp, scale=-math.pi / SEQ)
 
+        bps = psum.tile([P, DS], F32, name="bps", tag="hp")
+        nc.tensor.matmul(out=bps[:], lhsT=ones[:], rhs=brow[:], start=True, stop=True)
+        b_bc = const.tile([P, DS], F32, name="b_bc")
+        nc.vector.tensor_copy(out=b_bc[:], in_=bps[:])
+
+        bw_t = []
+
+        def build_bw(c):
+            bw = const.tile([P, 4, DS], F32, name="bw%d" % c)
+            for j in range(4):
+                col = wts[:, 4 * c + j : 4 * c + j + 1]
+                if c < BW_ON_VECTOR:
+                    nc.vector.tensor_scalar_mul(out=bw[:, j, :], in0=b_bc[:], scalar1=col)
+                else:
+                    nc.gpsimd.tensor_scalar(
+                        out=bw[:, j, :], in0=b_bc[:], scalar1=col, scalar2=0.0, op0=ALU.mult, op1=ALU.add
+                    )
+            bw_t.append(bw)
+
+        build_bw(0)
+
         w32 = w_sb[:].bitcast(F32)
         wt = psum.tile([P, 2, DS], F32, name="wt", tag="xt")
         for h in range(2):
@@ -105,24 +130,10 @@ def tile_attractorstate_v2_t_kernel(tc, hidden_states, positional_encodings, W, 
         wcodes = const.tile([P, DS], U32, name="wcodes", align_bytes=64)
         wscales = const.tile([P, DS], U8, name="wscales", align_bytes=64)
 
-        bps = psum.tile([P, DS], F32, name="bps", tag="hp")
-        nc.tensor.matmul(out=bps[:], lhsT=ones[:], rhs=brow[:], start=True, stop=True)
-        b_bc = const.tile([P, DS], F32, name="b_bc")
-        nc.vector.tensor_copy(out=b_bc[:], in_=bps[:])
+        build_bw(1)
         nc.vector.quantize_mx(out=wcodes[:].bitcast(FP8X4), scales=wscales[:], in_=wgrp[:])
-        bw_t = []
-        for c in range(CPB):
-            bw = const.tile([P, 4, DS], F32, name="bw%d" % c)
-            for j in range(4):
-                nc.gpsimd.tensor_scalar(
-                    out=bw[:, j, :],
-                    in0=b_bc[:],
-                    scalar1=wts[:, 4 * c + j : 4 * c + j + 1],
-                    scalar2=0.0,
-                    op0=ALU.mult,
-                    op1=ALU.add,
-                )
-            bw_t.append(bw)
+        for c in range(2, CPB):
+            build_bw(c)
 
         def ok(k):
             return 0 <= k < NCH
@@ -220,22 +231,44 @@ def tile_attractorstate_v2_t_kernel(tc, hidden_states, positional_encodings, W, 
             nc.vector.quantize_mx(out=gcodes[:].bitcast(FP8X4), scales=gscales[:], in_=ggrp_t[k][:])
             gq_t[k] = (gcodes, gscales)
 
+        def split(k):
+            return SPLIT if k >= G_FROM else SPLIT_EARLY
+
+        def pgrp_of(k):
+            if k not in pgrp_t:
+                pgrp_t[k] = work3.tile([P, 4 * DM], BF16, name="pgrp", align_bytes=64)
+            return pgrp_t[k]
+
         def st_RPs(k):
             if not ok(k):
                 return
-            pgrp = work3.tile([P, 4 * DM], BF16, name="pgrp", align_bytes=64)
-            pgrp_t[k] = pgrp
+            hi = split(k)[0] // 4
             nc.scalar.copy(
-                out=pgrp[:].rearrange("p (c i t) -> p c t i", i=4, t=4)[:, 0 : MS // 4],
-                in_=pe_t[k][:].rearrange("p (t c i) -> p c t i", t=4, i=4)[:, 0 : MS // 4],
+                out=pgrp_of(k)[:].rearrange("p (c i t) -> p c t i", i=4, t=4)[:, 0:hi],
+                in_=pe_t[k][:].rearrange("p (t c i) -> p c t i", t=4, i=4)[:, 0:hi],
             )
 
         def st_RPv(k):
             if not ok(k):
                 return
+            lo = split(k)[0] // 4
+            hi = (split(k)[0] + split(k)[1]) // 4
             nc.vector.tensor_copy(
-                out=pgrp_t[k][:].rearrange("p (c i t) -> p c t i", i=4, t=4)[:, MS // 4 : DM // 4],
-                in_=pe_t[k][:].rearrange("p (t c i) -> p c t i", t=4, i=4)[:, MS // 4 : DM // 4],
+                out=pgrp_of(k)[:].rearrange("p (c i t) -> p c t i", i=4, t=4)[:, lo:hi],
+                in_=pe_t[k][:].rearrange("p (t c i) -> p c t i", t=4, i=4)[:, lo:hi],
+            )
+
+        def st_RPg(k):
+            if not ok(k) or split(k)[2] == 0:
+                return
+            lo = DM - split(k)[2]
+            nc.gpsimd.tensor_scalar(
+                out=pgrp_of(k)[:].rearrange("p (m t) -> p m t", t=4)[:, lo:DM, :],
+                in0=pe_t[k][:].rearrange("p (t m) -> p m t", t=4)[:, lo:DM, :],
+                scalar1=1.0,
+                scalar2=0.0,
+                op0=ALU.mult,
+                op1=ALU.add,
             )
 
         def st_QP(k):
@@ -294,4 +327,5 @@ def tile_attractorstate_v2_t_kernel(tc, hidden_states, positional_encodings, W, 
             st_RPv(k + 1)
             st_RG(k)
             st_QP(k)
+            st_RPg(k + PGRP_BUFS)
             st_OUT(k - 1)

@@ -24,10 +24,7 @@ CHUNK = 512
 CPB = SEQ // CHUNK
 NCH = BATCH * CPB
 LOAD_AHEAD = 6
-SPLIT_EARLY = (240, 272, 0)
-SPLIT = (192, 176, 144)
-G_FROM = 4
-BW_ON_VECTOR = 4
+SPLIT = (176, 192, 144)
 PGRP_BUFS = 3
 
 
@@ -36,6 +33,7 @@ def tile_attractorstate_v2_t_kernel(tc, hidden_states, positional_encodings, W, 
     hs_flat = hidden_states.flatten_outer_dims()
     pe_flat = positional_encodings.flatten_outer_dims()
     out_flat = out.flatten_outer_dims()
+    step = math.pi / SEQ
 
     with ExitStack() as ctx:
         ctx.enter_context(tc.manual_schedule())
@@ -43,7 +41,7 @@ def tile_attractorstate_v2_t_kernel(tc, hidden_states, positional_encodings, W, 
         loads = ctx.enter_context(tc.tile_pool(name="loads", bufs=LOAD_AHEAD + 2))
         work2 = ctx.enter_context(tc.tile_pool(name="work2", bufs=2))
         work3 = ctx.enter_context(tc.tile_pool(name="work3", bufs=3))
-        psum = ctx.enter_context(tc.psum_pool(name="psum", bufs=2))
+        psum = ctx.enter_context(tc.psum_pool(name="psum", bufs=1))
 
         hs_t = {}
         pe_t = {}
@@ -58,85 +56,28 @@ def tile_attractorstate_v2_t_kernel(tc, hidden_states, positional_encodings, W, 
         pq_t = {}
         acc_t = {}
 
-        def load(k):
-            if k < 0 or k >= NCH:
-                return
-            rows = slice(k * CHUNK, (k + 1) * CHUNK)
-            hs_sb = loads.tile([P, 4 * DM], BF16, name="hs_sb")
-            nc.sync.dma_start(out=hs_sb[:], in_=hs_flat[rows, :].rearrange("(p j) d -> p (j d)", j=4))
-            pe_sb = loads.tile([P, 4 * DM], BF16, name="pe_sb")
-            nc.sync.dma_start(out=pe_sb[:], in_=pe_flat[rows, :].rearrange("(p j) d -> p (j d)", j=4))
-            hs_t[k] = hs_sb
-            pe_t[k] = pe_sb
-
-        w_sb = const.tile([P, 2 * DM], BF16, name="w_sb")
-        nc.sync.dma_start(
-            out=w_sb[:].rearrange("p (h d) -> p h d", h=2),
-            in_=W.rearrange("(h p) d -> p h d", p=P),
-        )
-        for k in range(LOAD_AHEAD):
-            load(k)
-
-        age_i = const.tile([P, 4 * CPB], I32, name="age_i")
-        nc.gpsimd.iota(age_i[:], pattern=[[-CHUNK, CPB], [-1, 4]], base=SEQ - 1, channel_multiplier=-4)
-        ident = const.tile([P, P], F32, name="ident")
-        make_identity(nc, ident[:])
-
-        ones = const.tile([P, P], BF16, name="ones")
-        nc.vector.memset(ones[:], 1.0)
-        brow = const.tile([P, DS], BF16, name="brow")
-        nc.vector.memset(brow[:], 0.0)
-        nc.scalar.dma_start(out=brow[0:1, :], in_=b.unsqueeze(0))
-        age_f = const.tile([P, 4 * CPB], F32, name="age_f")
-        nc.vector.tensor_copy(out=age_f[:], in_=age_i[:])
-        wts = const.tile([P, 4 * CPB], F32, name="wts")
-        nc.scalar.activation(out=wts[:], in_=age_f[:], func=ACT.Exp, scale=-math.pi / SEQ)
-
-        bps = psum.tile([P, DS], F32, name="bps", tag="hp")
-        nc.tensor.matmul(out=bps[:], lhsT=ones[:], rhs=brow[:], start=True, stop=True)
-        b_bc = const.tile([P, DS], F32, name="b_bc")
-        nc.vector.tensor_copy(out=b_bc[:], in_=bps[:])
-
-        bw_t = []
-
-        def build_bw(c):
-            bw = const.tile([P, 4, DS], F32, name="bw%d" % c)
-            for j in range(4):
-                col = wts[:, 4 * c + j : 4 * c + j + 1]
-                if c < BW_ON_VECTOR:
-                    nc.vector.tensor_scalar_mul(out=bw[:, j, :], in0=b_bc[:], scalar1=col)
-                else:
-                    nc.gpsimd.tensor_scalar(
-                        out=bw[:, j, :], in0=b_bc[:], scalar1=col, scalar2=0.0, op0=ALU.mult, op1=ALU.add
-                    )
-            bw_t.append(bw)
-
-        build_bw(0)
-
-        w32 = w_sb[:].bitcast(F32)
-        wt = psum.tile([P, 2, DS], F32, name="wt", tag="xt")
-        for h in range(2):
-            for u in range(2):
-                nc.tensor.transpose(
-                    wt[:, u, h * P : (h + 1) * P],
-                    w32[:, h * 256 + u * P : h * 256 + (u + 1) * P],
-                    ident[:],
-                )
-        wgrp = const.tile([P, 4 * DS], BF16, name="wgrp", align_bytes=64)
-        nc.vector.tensor_copy(
-            out=wgrp[:].bitcast(F32).rearrange("q (s u) -> q s u", u=2),
-            in_=wt[:].rearrange("q u s -> q s u"),
-        )
-        wcodes = const.tile([P, DS], U32, name="wcodes", align_bytes=64)
-        wscales = const.tile([P, DS], U8, name="wscales", align_bytes=64)
-
-        build_bw(1)
-        nc.vector.quantize_mx(out=wcodes[:].bitcast(FP8X4), scales=wscales[:], in_=wgrp[:])
-        for c in range(2, CPB):
-            build_bw(c)
-
         def ok(k):
             return 0 <= k < NCH
+
+        def load_hs(k):
+            if not ok(k):
+                return
+            hs_sb = loads.tile([P, 4 * DM], BF16, name="hs_sb")
+            nc.sync.dma_start(
+                out=hs_sb[:],
+                in_=hs_flat[k * CHUNK : (k + 1) * CHUNK, :].rearrange("(p j) d -> p (j d)", j=4),
+            )
+            hs_t[k] = hs_sb
+
+        def load_pe(k):
+            if not ok(k):
+                return
+            pe_sb = loads.tile([P, 4 * DM], BF16, name="pe_sb")
+            nc.sync.dma_start(
+                out=pe_sb[:],
+                in_=pe_flat[k * CHUNK : (k + 1) * CHUNK, :].rearrange("(p j) d -> p (j d)", j=4),
+            )
+            pe_t[k] = pe_sb
 
         def st_T(k):
             if not ok(k):
@@ -144,7 +85,7 @@ def tile_attractorstate_v2_t_kernel(tc, hidden_states, positional_encodings, W, 
             hs32 = hs_t[k][:].bitcast(F32)
             banks = []
             for a in range(2):
-                xt = psum.tile([P, 2, 2, P], F32, name="xt", tag="xt")
+                xt = psum.tile([P, 2, 2, P], F32, name="xt", tag="xt", bufs=2)
                 for jj in range(2):
                     j = 2 * a + jj
                     for u in range(2):
@@ -171,8 +112,8 @@ def tile_attractorstate_v2_t_kernel(tc, hidden_states, positional_encodings, W, 
         def st_QH(k):
             if not ok(k):
                 return
-            hcodes = work2.tile([P, CHUNK], U32, name="hcodes", align_bytes=64)
-            hscales = work2.tile([P, CHUNK], U8, name="hscales", align_bytes=64)
+            hcodes = work3.tile([P, CHUNK], U32, name="hcodes", align_bytes=64)
+            hscales = work3.tile([P, CHUNK], U8, name="hscales", align_bytes=64)
             nc.vector.quantize_mx(out=hcodes[:].bitcast(FP8X4), scales=hscales[:], in_=hgrp_t[k][:])
             hq_t[k] = (hcodes, hscales)
 
@@ -182,7 +123,7 @@ def tile_attractorstate_v2_t_kernel(tc, hidden_states, positional_encodings, W, 
             hcodes, hscales = hq_t[k]
             banks = []
             for a in range(2):
-                hp = psum.tile([P, 2, DS], F32, name="hp", tag="hp")
+                hp = psum.tile([P, 2, DS], F32, name="hp", tag="hp", bufs=4)
                 for jj in range(2):
                     j = 2 * a + jj
                     nc.tensor.matmul_mx(
@@ -197,17 +138,22 @@ def tile_attractorstate_v2_t_kernel(tc, hidden_states, positional_encodings, W, 
                 banks.append(hp)
             hp_t[k] = banks
 
+        def st_H(k):
+            st_A(k)
+            st_T(k + 1)
+            st_QH(k)
+            st_M1(k)
+
         def st_E(k):
             if not ok(k):
                 return
-            c = k % CPB
-            gj = work2.tile([P, 4, DS], BF16, name="gj")
+            gj = work2.tile([P, 4, DS], F32, name="gj")
             for j in range(4):
                 nc.vector.scalar_tensor_tensor(
                     out=gj[:, j, :],
                     in0=hp_t[k][j // 2][:, j % 2, :],
-                    scalar=wts[:, 4 * c + j : 4 * c + j + 1],
-                    in1=bw_t[c][:, j, :],
+                    scalar=math.exp(j * step),
+                    in1=b_j[:, j, :],
                     op0=ALU.mult,
                     op1=ALU.add,
                 )
@@ -216,33 +162,33 @@ def tile_attractorstate_v2_t_kernel(tc, hidden_states, positional_encodings, W, 
         def st_RG(k):
             if not ok(k):
                 return
+            c = k % CPB
             ggrp = work2.tile([P, 4 * DS], BF16, name="ggrp", align_bytes=64)
-            nc.scalar.copy(
+            nc.scalar.activation(
                 out=ggrp[:].rearrange("p (c i t) -> p c t i", i=4, t=4),
                 in_=gj_t[k][:].rearrange("p t (c i) -> p c t i", i=4),
+                func=ACT.Copy,
+                scale=wts[:, c : c + 1],
             )
             ggrp_t[k] = ggrp
 
         def st_QG(k):
             if not ok(k):
                 return
-            gcodes = work2.tile([P, DS], U32, name="gcodes", align_bytes=64)
-            gscales = work2.tile([P, DS], U8, name="gscales", align_bytes=64)
+            gcodes = work3.tile([P, DS], U32, name="gcodes", align_bytes=64)
+            gscales = work3.tile([P, DS], U8, name="gscales", align_bytes=64)
             nc.vector.quantize_mx(out=gcodes[:].bitcast(FP8X4), scales=gscales[:], in_=ggrp_t[k][:])
             gq_t[k] = (gcodes, gscales)
 
-        def split(k):
-            return SPLIT if k >= G_FROM else SPLIT_EARLY
-
         def pgrp_of(k):
             if k not in pgrp_t:
-                pgrp_t[k] = work3.tile([P, 4 * DM], BF16, name="pgrp", align_bytes=64)
+                pgrp_t[k] = work3.tile([P, 4 * DM], BF16, name="pgrp", align_bytes=64, bufs=PGRP_BUFS)
             return pgrp_t[k]
 
         def st_RPs(k):
             if not ok(k):
                 return
-            hi = split(k)[0] // 4
+            hi = SPLIT[0] // 4
             nc.scalar.copy(
                 out=pgrp_of(k)[:].rearrange("p (c i t) -> p c t i", i=4, t=4)[:, 0:hi],
                 in_=pe_t[k][:].rearrange("p (t c i) -> p c t i", t=4, i=4)[:, 0:hi],
@@ -251,17 +197,17 @@ def tile_attractorstate_v2_t_kernel(tc, hidden_states, positional_encodings, W, 
         def st_RPv(k):
             if not ok(k):
                 return
-            lo = split(k)[0] // 4
-            hi = (split(k)[0] + split(k)[1]) // 4
+            lo = SPLIT[0] // 4
+            hi = (SPLIT[0] + SPLIT[1]) // 4
             nc.vector.tensor_copy(
                 out=pgrp_of(k)[:].rearrange("p (c i t) -> p c t i", i=4, t=4)[:, lo:hi],
                 in_=pe_t[k][:].rearrange("p (t c i) -> p c t i", t=4, i=4)[:, lo:hi],
             )
 
         def st_RPg(k):
-            if not ok(k) or split(k)[2] == 0:
+            if not ok(k):
                 return
-            lo = DM - split(k)[2]
+            lo = DM - SPLIT[2]
             nc.gpsimd.tensor_scalar(
                 out=pgrp_of(k)[:].rearrange("p (m t) -> p m t", t=4)[:, lo:DM, :],
                 in0=pe_t[k][:].rearrange("p (t m) -> p m t", t=4)[:, lo:DM, :],
@@ -314,18 +260,74 @@ def tile_attractorstate_v2_t_kernel(tc, hidden_states, positional_encodings, W, 
                 r0 = i * DS + h * P
                 nc.sync.dma_start(out=out_flat[r0 : r0 + P, :], in_=o_sb[:])
 
-        for k in range(-2, NCH + 1):
-            load(k + LOAD_AHEAD + 2)
+        brow = const.tile([P, DS], BF16, name="brow")
+        nc.vector.memset(brow[:], 0.0)
+        ones = const.tile([P, P], BF16, name="ones")
+        nc.vector.memset(ones[:], 1.0)
+
+        w_sb = const.tile([P, 2 * DM], BF16, name="w_sb")
+        nc.sync.dma_start(
+            out=w_sb[:].rearrange("p (h d) -> p h d", h=2),
+            in_=W.rearrange("(h p) d -> p h d", p=P),
+        )
+        load_hs(0)
+        nc.sync.dma_start(out=brow[0:1, :], in_=b.unsqueeze(0))
+        load_hs(1)
+        load_pe(0)
+        load_pe(1)
+        for k in range(2, LOAD_AHEAD):
+            load_hs(k)
+            load_pe(k)
+
+        age_i = const.tile([P, CPB], I32, name="age_i")
+        nc.gpsimd.iota(age_i[:], pattern=[[-CHUNK, CPB]], base=SEQ - 1, channel_multiplier=-4)
+        ident = const.tile([P, P], F32, name="ident")
+        make_identity(nc, ident[:])
+        age_f = const.tile([P, CPB], F32, name="age_f")
+        nc.vector.tensor_copy(out=age_f[:], in_=age_i[:])
+        wts = const.tile([P, CPB], F32, name="wts")
+        nc.scalar.activation(out=wts[:], in_=age_f[:], func=ACT.Exp, scale=-step)
+
+        w32 = w_sb[:].bitcast(F32)
+        wt = psum.tile([P, 2, DS], F32, name="wt", tag="xt", bufs=2)
+        for h in range(2):
+            for u in range(2):
+                nc.tensor.transpose(
+                    wt[:, u, h * P : (h + 1) * P],
+                    w32[:, h * 256 + u * P : h * 256 + (u + 1) * P],
+                    ident[:],
+                )
+        wgrp = const.tile([P, 4 * DS], BF16, name="wgrp", align_bytes=64)
+        nc.vector.tensor_copy(
+            out=wgrp[:].bitcast(F32).rearrange("q (s u) -> q s u", u=2),
+            in_=wt[:].rearrange("q u s -> q s u"),
+        )
+        wcodes = const.tile([P, DS], U32, name="wcodes", align_bytes=64)
+        wscales = const.tile([P, DS], U8, name="wscales", align_bytes=64)
+        st_T(0)
+        bps = psum.tile([P, DS], F32, name="bps", tag="acc0")
+        nc.tensor.matmul(out=bps[:], lhsT=ones[:], rhs=brow[:], start=True, stop=True)
+        st_RPg(0)
+        st_RPg(1)
+        nc.vector.quantize_mx(out=wcodes[:].bitcast(FP8X4), scales=wscales[:], in_=wgrp[:])
+        st_H(0)
+        b_j = const.tile([P, 4, DS], F32, name="b_j")
+        for j in range(4):
+            nc.vector.tensor_scalar_mul(out=b_j[:, j, :], in0=bps[:], scalar1=math.exp(j * step))
+        st_RPv(0)
+        st_RPs(0)
+        st_H(1)
+
+        for k in range(NCH + 2):
+            load_hs(k + LOAD_AHEAD)
+            load_pe(k + LOAD_AHEAD)
+            st_M2(k - 2)
             st_E(k)
-            st_A(k + 1)
-            st_T(k + 2)
-            st_QG(k - 1)
-            st_M2(k - 1)
+            st_OUT(k - 2)
+            st_H(k + 2)
             st_RPs(k + 1)
-            st_QH(k + 1)
-            st_M1(k + 1)
             st_RPv(k + 1)
             st_RG(k)
-            st_QP(k)
-            st_RPg(k + PGRP_BUFS)
-            st_OUT(k - 1)
+            st_QP(k - 1)
+            st_QG(k - 1)
+            st_RPg(k + 2)

@@ -138,12 +138,6 @@ def tile_attractorstate_v2_t_kernel(tc, hidden_states, positional_encodings, W, 
                 banks.append(hp)
             hp_t[k] = banks
 
-        def st_H(k):
-            st_A(k)
-            st_T(k + 1)
-            st_QH(k)
-            st_M1(k)
-
         def st_E(k):
             if not ok(k):
                 return
@@ -272,8 +266,8 @@ def tile_attractorstate_v2_t_kernel(tc, hidden_states, positional_encodings, W, 
         )
         load_hs(0)
         nc.sync.dma_start(out=brow[0:1, :], in_=b.unsqueeze(0))
-        load_hs(1)
         load_pe(0)
+        load_hs(1)
         load_pe(1)
         for k in range(2, LOAD_AHEAD):
             load_hs(k)
@@ -307,27 +301,45 @@ def tile_attractorstate_v2_t_kernel(tc, hidden_states, positional_encodings, W, 
         st_T(0)
         bps = psum.tile([P, DS], F32, name="bps", tag="acc0")
         nc.tensor.matmul(out=bps[:], lhsT=ones[:], rhs=brow[:], start=True, stop=True)
-        st_RPg(0)
-        st_RPg(1)
+        for k in range(PGRP_BUFS):
+            st_RPg(k)
         nc.vector.quantize_mx(out=wcodes[:].bitcast(FP8X4), scales=wscales[:], in_=wgrp[:])
-        st_H(0)
+        st_RPv(0)
         b_j = const.tile([P, 4, DS], F32, name="b_j")
         for j in range(4):
             nc.vector.tensor_scalar_mul(out=b_j[:, j, :], in0=bps[:], scalar1=math.exp(j * step))
-        st_RPv(0)
+        st_A(0)
+        st_T(1)
+        st_QH(0)
+        st_M1(0)
         st_RPs(0)
-        st_H(1)
+        st_QP(0)
+        st_A(1)
+        st_T(2)
 
         for k in range(NCH + 2):
             load_hs(k + LOAD_AHEAD)
             load_pe(k + LOAD_AHEAD)
-            st_M2(k - 2)
-            st_E(k)
+            if k != NCH - 1:
+                st_E(k)
+            if k == NCH - 2:
+                st_E(k + 1)
+            if k == 0:
+                st_QH(1)
+                st_M1(1)
             st_OUT(k - 2)
-            st_H(k + 2)
+            st_QG(k - 1)
+            st_M2(k - 1)
             st_RPs(k + 1)
             st_RPv(k + 1)
-            st_RG(k)
-            st_QP(k - 1)
-            st_QG(k - 1)
-            st_RPg(k + 2)
+            st_A(k + 2)
+            st_T(k + 3)
+            if k != NCH - 1:
+                st_RG(k)
+            if k == NCH - 2:
+                st_RG(k + 1)
+            st_QH(k + 2)
+            st_M1(k + 2)
+            if k > 0:
+                st_QP(k)
+            st_RPg(k + PGRP_BUFS)

@@ -338,8 +338,8 @@ def tile_attractorstate_v2_t_kernel(tc, hidden_states, positional_encodings, W, 
                 st_RG(k)
             if k == NCH - 2:
                 st_RG(k + 1)
-            st_QH(k + 2)
-            st_M1(k + 2)
             if k > 0:
                 st_QP(k)
             st_RPg(k + PGRP_BUFS)
+            st_QH(k + 2)
+            st_M1(k + 2)

@@ -24,7 +24,7 @@ CHUNK = 512
 CPB = SEQ // CHUNK
 NCH = BATCH * CPB
 LOAD_AHEAD = 6
-SPLIT = (176, 192, 144)
+SPLIT = (184, 168, 160)
 PGRP_BUFS = 3
 
 
@@ -247,7 +247,7 @@ def tile_attractorstate_v2_t_kernel(tc, hidden_states, positional_encodings, W, 
             i = k // CPB
             for h in range(2):
                 o_sb = work2.tile([P, DM], F32, name="o_sb%d" % h)
-                if h == 0:
+                if h == 0 and i == BATCH - 1:
                     nc.vector.tensor_copy(out=o_sb[:], in_=acc_t[i][h][:])
                 else:
                     nc.scalar.copy(out=o_sb[:], in_=acc_t[i][h][:])

@@ -247,7 +247,7 @@ def tile_attractorstate_v2_t_kernel(tc, hidden_states, positional_encodings, W, 
             i = k // CPB
             for h in range(2):
                 o_sb = work2.tile([P, DM], F32, name="o_sb%d" % h)
-                if h == 0 and i == BATCH - 1:
+                if h == 0:
                     nc.vector.tensor_copy(out=o_sb[:], in_=acc_t[i][h][:])
                 else:
                     nc.scalar.copy(out=o_sb[:], in_=acc_t[i][h][:])

@@ -24,7 +24,7 @@ CHUNK = 512
 CPB = SEQ // CHUNK
 NCH = BATCH * CPB
 LOAD_AHEAD = 6
-SPLIT = (184, 168, 160)
+SPLIT = (256, 64, 192)
 PGRP_BUFS = 3
 
 
@@ -49,7 +49,8 @@ def tile_attractorstate_v2_t_kernel(tc, hidden_states, positional_encodings, W, 
         hgrp_t = {}
         hq_t = {}
         hp_t = {}
-        gj_t = {}
+        gt_t = {}
+        gps_t = {}
         ggrp_t = {}
         gq_t = {}
         pgrp_t = {}
@@ -101,11 +102,11 @@ def tile_attractorstate_v2_t_kernel(tc, hidden_states, positional_encodings, W, 
             if not ok(k):
                 return
             hgrp = work2.tile([P, 4 * CHUNK], BF16, name="hgrp", align_bytes=64)
-            h32 = hgrp[:].bitcast(F32).rearrange("q (a t u) -> q a t u", a=4, u=2)
+            h32 = hgrp[:].bitcast(F32).rearrange("q (a t j u) -> q a t j u", a=2, j=2, u=2)
             for a in range(2):
                 nc.scalar.copy(
-                    out=h32[:, 2 * a : 2 * a + 2, :, :],
-                    in_=xt_t[k][a][:].rearrange("q a u t -> q a t u"),
+                    out=h32[:, a, :, :, :],
+                    in_=xt_t[k][a][:].rearrange("q j u t -> q t j u"),
                 )
             hgrp_t[k] = hgrp
 
@@ -122,47 +123,57 @@ def tile_attractorstate_v2_t_kernel(tc, hidden_states, positional_encodings, W, 
                 return
             hcodes, hscales = hq_t[k]
             banks = []
-            for a in range(2):
-                hp = psum.tile([P, 2, DS], F32, name="hp", tag="hp", bufs=4)
-                for jj in range(2):
-                    j = 2 * a + jj
-                    nc.tensor.matmul_mx(
-                        out=hp[:, jj, :],
-                        lhsT=hcodes[:, j * P : (j + 1) * P].bitcast(FP8X4),
-                        lhsT_scale=hscales[:, j * P : (j + 1) * P],
-                        rhs=wcodes[:].bitcast(FP8X4),
-                        rhs_scale=wscales[:],
-                        start=True,
-                        stop=True,
-                    )
+            for h in range(2):
+                hp = psum.tile([P, CHUNK], F32, name="hp", tag="hp", bufs=3)
+                nc.tensor.matmul_mx(
+                    out=hp[:],
+                    lhsT=wcodes[:, h * P : (h + 1) * P].bitcast(FP8X4),
+                    lhsT_scale=wscales[:, h * P : (h + 1) * P],
+                    rhs=hcodes[:].bitcast(FP8X4),
+                    rhs_scale=hscales[:],
+                    start=True,
+                    stop=True,
+                )
                 banks.append(hp)
             hp_t[k] = banks
 
         def st_E(k):
             if not ok(k):
                 return
-            gj = work2.tile([P, 4, DS], F32, name="gj")
-            for j in range(4):
+            c = k % CPB
+            gt = work2.tile([P, 2, CHUNK], BF16, name="gt")
+            for h in range(2):
                 nc.vector.scalar_tensor_tensor(
-                    out=gj[:, j, :],
-                    in0=hp_t[k][j // 2][:, j % 2, :],
-                    scalar=math.exp(j * step),
-                    in1=b_j[:, j, :],
-                    op0=ALU.mult,
-                    op1=ALU.add,
+                    out=gt[:, h, :],
+                    in0=hp_t[k][h][:],
+                    scalar=bcol[:, h : h + 1],
+                    in1=wtab[:, c * CHUNK : (c + 1) * CHUNK],
+                    op0=ALU.add,
+                    op1=ALU.mult,
                 )
-            gj_t[k] = gj
+            gt_t[k] = gt
+
+        def st_TG(k):
+            if not ok(k):
+                return
+            g32 = gt_t[k][:].rearrange("s h n -> s (h n)").bitcast(F32)
+            gps = psum.tile([P, 2, DS], F32, name="gps", tag="gps")
+            for h in range(2):
+                for a in range(2):
+                    nc.tensor.transpose(
+                        gps[:, a, h * P : (h + 1) * P],
+                        g32[:, h * 256 + a * P : h * 256 + (a + 1) * P],
+                        ident[:],
+                    )
+            gps_t[k] = gps
 
         def st_RG(k):
             if not ok(k):
                 return
-            c = k % CPB
             ggrp = work2.tile([P, 4 * DS], BF16, name="ggrp", align_bytes=64)
-            nc.scalar.activation(
-                out=ggrp[:].rearrange("p (c i t) -> p c t i", i=4, t=4),
-                in_=gj_t[k][:].rearrange("p t (c i) -> p c t i", i=4),
-                func=ACT.Copy,
-                scale=wts[:, c : c + 1],
+            nc.scalar.copy(
+                out=ggrp[:].bitcast(F32).rearrange("p (s a) -> p s a", a=2),
+                in_=gps_t[k][:].rearrange("p a s -> p s a"),
             )
             ggrp_t[k] = ggrp
 
@@ -201,10 +212,10 @@ def tile_attractorstate_v2_t_kernel(tc, hidden_states, positional_encodings, W, 
         def st_RPg(k):
             if not ok(k):
                 return
-            lo = DM - SPLIT[2]
+            lo = (DM - SPLIT[2]) // 4
             nc.gpsimd.tensor_scalar(
-                out=pgrp_of(k)[:].rearrange("p (m t) -> p m t", t=4)[:, lo:DM, :],
-                in0=pe_t[k][:].rearrange("p (t m) -> p m t", t=4)[:, lo:DM, :],
+                out=pgrp_of(k)[:].rearrange("p (c i t) -> p c t i", i=4, t=4)[:, lo:],
+                in0=pe_t[k][:].rearrange("p (t c i) -> p c t i", t=4, i=4)[:, lo:],
                 scalar1=1.0,
                 scalar2=0.0,
                 op0=ALU.mult,
@@ -256,7 +267,7 @@ def tile_attractorstate_v2_t_kernel(tc, hidden_states, positional_encodings, W, 
 
         brow = const.tile([P, DS], BF16, name="brow")
         nc.vector.memset(brow[:], 0.0)
-        ones = const.tile([P, P], BF16, name="ones")
+        ones = const.tile([P, 32], BF16, name="ones")
         nc.vector.memset(ones[:], 1.0)
 
         w_sb = const.tile([P, 2 * DM], BF16, name="w_sb")
@@ -273,14 +284,23 @@ def tile_attractorstate_v2_t_kernel(tc, hidden_states, positional_encodings, W, 
             load_hs(k)
             load_pe(k)
 
-        age_i = const.tile([P, CPB], I32, name="age_i")
-        nc.gpsimd.iota(age_i[:], pattern=[[-CHUNK, CPB]], base=SEQ - 1, channel_multiplier=-4)
         ident = const.tile([P, P], F32, name="ident")
         make_identity(nc, ident[:])
-        age_f = const.tile([P, CPB], F32, name="age_f")
+        age_i = const.tile([P, CHUNK], I32, name="age_i")
+        nc.gpsimd.iota(age_i[:], pattern=[[-2, 2], [-4, P], [-1, 2]], base=CHUNK - 1, channel_multiplier=0)
+        age_f = const.tile([P, CHUNK], F32, name="age_f")
         nc.vector.tensor_copy(out=age_f[:], in_=age_i[:])
-        wts = const.tile([P, CPB], F32, name="wts")
-        nc.scalar.activation(out=wts[:], in_=age_f[:], func=ACT.Exp, scale=-step)
+        wtab = const.tile([P, SEQ], F32, name="wtab")
+        nc.scalar.activation(out=wtab[:, SEQ - CHUNK : SEQ], in_=age_f[:], func=ACT.Exp, scale=-step)
+        for c in range(CPB - 1):
+            nc.gpsimd.tensor_scalar(
+                out=wtab[:, c * CHUNK : (c + 1) * CHUNK],
+                in0=wtab[:, SEQ - CHUNK : SEQ],
+                scalar1=math.exp(-step * CHUNK * (CPB - 1 - c)),
+                scalar2=0.0,
+                op0=ALU.mult,
+                op1=ALU.add,
+            )
 
         w32 = w_sb[:].bitcast(F32)
         wt = psum.tile([P, 2, DS], F32, name="wt", tag="xt", bufs=2)
@@ -299,15 +319,17 @@ def tile_attractorstate_v2_t_kernel(tc, hidden_states, positional_encodings, W, 
         wcodes = const.tile([P, DS], U32, name="wcodes", align_bytes=64)
         wscales = const.tile([P, DS], U8, name="wscales", align_bytes=64)
         st_T(0)
-        bps = psum.tile([P, DS], F32, name="bps", tag="acc0")
-        nc.tensor.matmul(out=bps[:], lhsT=ones[:], rhs=brow[:], start=True, stop=True)
+        bps = psum.tile([P, 2, 32], F32, name="bps", tag="gps")
+        for h in range(2):
+            nc.tensor.matmul(
+                out=bps[:, h, :], lhsT=brow[:, h * P : (h + 1) * P], rhs=ones[:], start=True, stop=True
+            )
         for k in range(PGRP_BUFS):
             st_RPg(k)
         nc.vector.quantize_mx(out=wcodes[:].bitcast(FP8X4), scales=wscales[:], in_=wgrp[:])
         st_RPv(0)
-        b_j = const.tile([P, 4, DS], F32, name="b_j")
-        for j in range(4):
-            nc.vector.tensor_scalar_mul(out=b_j[:, j, :], in0=bps[:], scalar1=math.exp(j * step))
+        bcol = const.tile([P, 2], F32, name="bcol")
+        nc.vector.tensor_copy(out=bcol[:], in_=bps[:, :, 0])
         st_A(0)
         st_T(1)
         st_QH(0)
@@ -320,26 +342,20 @@ def tile_attractorstate_v2_t_kernel(tc, hidden_states, positional_encodings, W, 
         for k in range(NCH + 2):
             load_hs(k + LOAD_AHEAD)
             load_pe(k + LOAD_AHEAD)
-            if k != NCH - 1:
-                st_E(k)
-            if k == NCH - 2:
-                st_E(k + 1)
+            st_E(k)
             if k == 0:
                 st_QH(1)
-                st_M1(1)
+            st_M1(k + 1)
             st_OUT(k - 2)
             st_QG(k - 1)
+            st_A(k + 2)
+            st_TG(k)
+            st_T(k + 3)
             st_M2(k - 1)
             st_RPs(k + 1)
+            st_RG(k)
             st_RPv(k + 1)
-            st_A(k + 2)
-            st_T(k + 3)
-            if k != NCH - 1:
-                st_RG(k)
-            if k == NCH - 2:
-                st_RG(k + 1)
             if k > 0:
                 st_QP(k)
             st_RPg(k + PGRP_BUFS)
             st_QH(k + 2)
-            st_M1(k + 2)

@@ -24,8 +24,10 @@ CHUNK = 512
 CPB = SEQ // CHUNK
 NCH = BATCH * CPB
 LOAD_AHEAD = 6
-SPLIT = (256, 64, 192)
-PGRP_BUFS = 3
+S_COLS = 272
+V_COLS = 64
+G_COLS = 176
+Q_BUFS = 3
 
 
 def tile_attractorstate_v2_t_kernel(tc, hidden_states, positional_encodings, W, b, out):
@@ -46,28 +48,29 @@ def tile_attractorstate_v2_t_kernel(tc, hidden_states, positional_encodings, W, 
         hs_t = {}
         pe_t = {}
         xt_t = {}
-        hgrp_t = {}
+        h_in = {}
         hq_t = {}
         hp_t = {}
         gt_t = {}
         gps_t = {}
         ggrp_t = {}
         gq_t = {}
-        pgrp_t = {}
+        q_in = {}
         pq_t = {}
         acc_t = {}
+        pi_t = {}
 
         def ok(k):
             return 0 <= k < NCH
 
-        def load_hs(k):
+        def load_hs(k, parts=1):
             if not ok(k):
                 return
             hs_sb = loads.tile([P, 4 * DM], BF16, name="hs_sb")
-            nc.sync.dma_start(
-                out=hs_sb[:],
-                in_=hs_flat[k * CHUNK : (k + 1) * CHUNK, :].rearrange("(p j) d -> p (j d)", j=4),
-            )
+            view = hs_flat[k * CHUNK : (k + 1) * CHUNK, :].rearrange("(p j) d -> p (j d)", j=4)
+            w = 4 * DM // parts
+            for i in range(parts):
+                nc.sync.dma_start(out=hs_sb[:, i * w : (i + 1) * w], in_=view[:, i * w : (i + 1) * w])
             hs_t[k] = hs_sb
 
         def load_pe(k):
@@ -79,6 +82,21 @@ def tile_attractorstate_v2_t_kernel(tc, hidden_states, positional_encodings, W, 
                 in_=pe_flat[k * CHUNK : (k + 1) * CHUNK, :].rearrange("(p j) d -> p (j d)", j=4),
             )
             pe_t[k] = pe_sb
+
+        def q_of(k):
+            if k not in q_in:
+                q_in[k] = work3.tile([P, 8 * DM], BF16, name="q_in", align_bytes=64, bufs=Q_BUFS)
+            return q_in[k]
+
+        def pgrp_of(k):
+            return q_of(k)[:, 0 : 4 * DM]
+
+        def hgrp_of(k):
+            if k >= 2:
+                return q_of(k - 2)[:, 4 * DM : 8 * DM]
+            if k not in h_in:
+                h_in[k] = const.tile([P, 4 * CHUNK], BF16, name="h_in%d" % k, align_bytes=64)
+            return h_in[k][:]
 
         def st_T(k):
             if not ok(k):
@@ -101,22 +119,30 @@ def tile_attractorstate_v2_t_kernel(tc, hidden_states, positional_encodings, W, 
         def st_A(k):
             if not ok(k):
                 return
-            hgrp = work2.tile([P, 4 * CHUNK], BF16, name="hgrp", align_bytes=64)
-            h32 = hgrp[:].bitcast(F32).rearrange("q (a t j u) -> q a t j u", a=2, j=2, u=2)
+            h32 = hgrp_of(k).bitcast(F32).rearrange("q (a t j u) -> q a t j u", a=2, j=2, u=2)
             for a in range(2):
                 nc.scalar.copy(
                     out=h32[:, a, :, :, :],
                     in_=xt_t[k][a][:].rearrange("q j u t -> q t j u"),
                 )
-            hgrp_t[k] = hgrp
 
         def st_QH(k):
+            hcodes = const.tile([P, CHUNK], U32, name="hcodes%d" % k, align_bytes=64)
+            hscales = const.tile([P, CHUNK], U8, name="hscales%d" % k, align_bytes=64)
+            nc.vector.quantize_mx(out=hcodes[:].bitcast(FP8X4), scales=hscales[:], in_=hgrp_of(k))
+            hq_t[k] = (hcodes[:], hscales[:])
+
+        def st_Q(k):
             if not ok(k):
                 return
-            hcodes = work3.tile([P, CHUNK], U32, name="hcodes", align_bytes=64)
-            hscales = work3.tile([P, CHUNK], U8, name="hscales", align_bytes=64)
-            nc.vector.quantize_mx(out=hcodes[:].bitcast(FP8X4), scales=hscales[:], in_=hgrp_t[k][:])
-            hq_t[k] = (hcodes, hscales)
+            codes = work3.tile([P, 2 * DM], U32, name="codes", align_bytes=64)
+            scales = work3.tile([P, 2 * DM], U8, name="scales", align_bytes=64)
+            w = 2 * DM if ok(k + 2) else DM
+            nc.vector.quantize_mx(
+                out=codes[:, 0:w].bitcast(FP8X4), scales=scales[:, 0:w], in_=q_of(k)[:, 0 : 4 * w]
+            )
+            pq_t[k] = (codes[:, 0:DM], scales[:, 0:DM])
+            hq_t[k + 2] = (codes[:, DM : 2 * DM], scales[:, DM : 2 * DM])
 
         def st_M1(k):
             if not ok(k):
@@ -129,8 +155,8 @@ def tile_attractorstate_v2_t_kernel(tc, hidden_states, positional_encodings, W, 
                     out=hp[:],
                     lhsT=wcodes[:, h * P : (h + 1) * P].bitcast(FP8X4),
                     lhsT_scale=wscales[:, h * P : (h + 1) * P],
-                    rhs=hcodes[:].bitcast(FP8X4),
-                    rhs_scale=hscales[:],
+                    rhs=hcodes.bitcast(FP8X4),
+                    rhs_scale=hscales,
                     start=True,
                     stop=True,
                 )
@@ -185,50 +211,36 @@ def tile_attractorstate_v2_t_kernel(tc, hidden_states, positional_encodings, W, 
             nc.vector.quantize_mx(out=gcodes[:].bitcast(FP8X4), scales=gscales[:], in_=ggrp_t[k][:])
             gq_t[k] = (gcodes, gscales)
 
-        def pgrp_of(k):
-            if k not in pgrp_t:
-                pgrp_t[k] = work3.tile([P, 4 * DM], BF16, name="pgrp", align_bytes=64, bufs=PGRP_BUFS)
-            return pgrp_t[k]
-
         def st_RPs(k):
             if not ok(k):
                 return
-            hi = SPLIT[0] // 4
             nc.scalar.copy(
-                out=pgrp_of(k)[:].rearrange("p (c i t) -> p c t i", i=4, t=4)[:, 0:hi],
-                in_=pe_t[k][:].rearrange("p (t c i) -> p c t i", t=4, i=4)[:, 0:hi],
+                out=pgrp_of(k).rearrange("p (c i t) -> p c t i", i=4, t=4)[:, 0 : S_COLS // 4],
+                in_=pe_t[k][:].rearrange("p (t c i) -> p c t i", t=4, i=4)[:, 0 : S_COLS // 4],
             )
 
         def st_RPv(k):
             if not ok(k):
                 return
-            lo = SPLIT[0] // 4
-            hi = (SPLIT[0] + SPLIT[1]) // 4
+            lo = (DM - G_COLS - V_COLS) // 4
+            hi = (DM - G_COLS) // 4
             nc.vector.tensor_copy(
-                out=pgrp_of(k)[:].rearrange("p (c i t) -> p c t i", i=4, t=4)[:, lo:hi],
+                out=pgrp_of(k).rearrange("p (c i t) -> p c t i", i=4, t=4)[:, lo:hi],
                 in_=pe_t[k][:].rearrange("p (t c i) -> p c t i", t=4, i=4)[:, lo:hi],
             )
 
         def st_RPg(k):
             if not ok(k):
                 return
-            lo = (DM - SPLIT[2]) // 4
+            lo = (DM - G_COLS) // 4
             nc.gpsimd.tensor_scalar(
-                out=pgrp_of(k)[:].rearrange("p (c i t) -> p c t i", i=4, t=4)[:, lo:],
+                out=pgrp_of(k).rearrange("p (c i t) -> p c t i", i=4, t=4)[:, lo:],
                 in0=pe_t[k][:].rearrange("p (t c i) -> p c t i", t=4, i=4)[:, lo:],
                 scalar1=1.0,
                 scalar2=0.0,
                 op0=ALU.mult,
                 op1=ALU.add,
             )
-
-        def st_QP(k):
-            if not ok(k):
-                return
-            pcodes = work3.tile([P, DM], U32, name="pcodes", align_bytes=64)
-            pscales = work3.tile([P, DM], U8, name="pscales", align_bytes=64)
-            nc.vector.quantize_mx(out=pcodes[:].bitcast(FP8X4), scales=pscales[:], in_=pgrp_t[k][:])
-            pq_t[k] = (pcodes, pscales)
 
         def st_M2(k):
             if not ok(k):
@@ -246,8 +258,8 @@ def tile_attractorstate_v2_t_kernel(tc, hidden_states, positional_encodings, W, 
                     out=acc_t[i][h][:],
                     lhsT=gcodes[:, h * P : (h + 1) * P].bitcast(FP8X4),
                     lhsT_scale=gscales[:, h * P : (h + 1) * P],
-                    rhs=pcodes[:].bitcast(FP8X4),
-                    rhs_scale=pscales[:],
+                    rhs=pcodes.bitcast(FP8X4),
+                    rhs_scale=pscales,
                     start=(c == 0),
                     stop=(c == CPB - 1),
                 )
@@ -265,41 +277,36 @@ def tile_attractorstate_v2_t_kernel(tc, hidden_states, positional_encodings, W, 
                 r0 = i * DS + h * P
                 nc.sync.dma_start(out=out_flat[r0 : r0 + P, :], in_=o_sb[:])
 
-        brow = const.tile([P, DS], BF16, name="brow")
-        nc.vector.memset(brow[:], 0.0)
-        ones = const.tile([P, 32], BF16, name="ones")
-        nc.vector.memset(ones[:], 1.0)
-
         w_sb = const.tile([P, 2 * DM], BF16, name="w_sb")
         nc.sync.dma_start(
             out=w_sb[:].rearrange("p (h d) -> p h d", h=2),
             in_=W.rearrange("(h p) d -> p h d", p=P),
         )
-        load_hs(0)
+        load_hs(0, parts=2)
+        brow = const.tile([P, DS], BF16, name="brow")
+        nc.vector.memset(brow[:], 0.0)
         nc.sync.dma_start(out=brow[0:1, :], in_=b.unsqueeze(0))
-        load_pe(0)
         load_hs(1)
-        load_pe(1)
+        load_pe(0)
         for k in range(2, LOAD_AHEAD):
             load_hs(k)
-            load_pe(k)
+            load_pe(k - 1)
+        ones = const.tile([P, 32], BF16, name="ones")
+        nc.vector.memset(ones[:], 1.0)
 
-        ident = const.tile([P, P], F32, name="ident")
-        make_identity(nc, ident[:])
         age_i = const.tile([P, CHUNK], I32, name="age_i")
         nc.gpsimd.iota(age_i[:], pattern=[[-2, 2], [-4, P], [-1, 2]], base=CHUNK - 1, channel_multiplier=0)
+        ident = const.tile([P, P], F32, name="ident")
+        make_identity(nc, ident[:])
         age_f = const.tile([P, CHUNK], F32, name="age_f")
         nc.vector.tensor_copy(out=age_f[:], in_=age_i[:])
         wtab = const.tile([P, SEQ], F32, name="wtab")
         nc.scalar.activation(out=wtab[:, SEQ - CHUNK : SEQ], in_=age_f[:], func=ACT.Exp, scale=-step)
         for c in range(CPB - 1):
-            nc.gpsimd.tensor_scalar(
+            nc.vector.tensor_scalar_mul(
                 out=wtab[:, c * CHUNK : (c + 1) * CHUNK],
                 in0=wtab[:, SEQ - CHUNK : SEQ],
                 scalar1=math.exp(-step * CHUNK * (CPB - 1 - c)),
-                scalar2=0.0,
-                op0=ALU.mult,
-                op1=ALU.add,
             )
 
         w32 = w_sb[:].bitcast(F32)
@@ -324,38 +331,36 @@ def tile_attractorstate_v2_t_kernel(tc, hidden_states, positional_encodings, W, 
             nc.tensor.matmul(
                 out=bps[:, h, :], lhsT=brow[:, h * P : (h + 1) * P], rhs=ones[:], start=True, stop=True
             )
-        for k in range(PGRP_BUFS):
-            st_RPg(k)
         nc.vector.quantize_mx(out=wcodes[:].bitcast(FP8X4), scales=wscales[:], in_=wgrp[:])
-        st_RPv(0)
         bcol = const.tile([P, 2], F32, name="bcol")
         nc.vector.tensor_copy(out=bcol[:], in_=bps[:, :, 0])
         st_A(0)
         st_T(1)
         st_QH(0)
         st_M1(0)
-        st_RPs(0)
-        st_QP(0)
         st_A(1)
         st_T(2)
+        st_QH(1)
+        for k in range(Q_BUFS):
+            st_RPg(k)
+        st_A(2)
+        st_RPs(0)
+        st_RPv(0)
+        st_RPs(1)
 
         for k in range(NCH + 2):
             load_hs(k + LOAD_AHEAD)
-            load_pe(k + LOAD_AHEAD)
+            load_pe(k + LOAD_AHEAD - 1)
             st_E(k)
-            if k == 0:
-                st_QH(1)
             st_M1(k + 1)
             st_OUT(k - 2)
             st_QG(k - 1)
-            st_A(k + 2)
             st_TG(k)
             st_T(k + 3)
-            st_M2(k - 1)
-            st_RPs(k + 1)
             st_RG(k)
+            st_A(k + 3)
+            st_M2(k - 1)
             st_RPv(k + 1)
-            if k > 0:
-                st_QP(k)
-            st_RPg(k + PGRP_BUFS)
-            st_QH(k + 2)
+            st_Q(k)
+            st_RPs(k + 2)
+            st_RPg(k + Q_BUFS)

@@ -25,9 +25,10 @@ CPB = SEQ // CHUNK
 NCH = BATCH * CPB
 LOAD_AHEAD = 6
 S_COLS = 272
-V_COLS = 64
-G_COLS = 176
+V_COLS = 56
+G_COLS = 184
 Q_BUFS = 3
+G_FROM = 4
 
 
 def tile_attractorstate_v2_t_kernel(tc, hidden_states, positional_encodings, W, b, out):
@@ -135,8 +136,8 @@ def tile_attractorstate_v2_t_kernel(tc, hidden_states, positional_encodings, W, 
         def st_Q(k):
             if not ok(k):
                 return
-            codes = work3.tile([P, 2 * DM], U32, name="codes", align_bytes=64)
-            scales = work3.tile([P, 2 * DM], U8, name="scales", align_bytes=64)
+            codes = work3.tile([P, 2 * DM], U32, name="codes", align_bytes=64, bufs=4)
+            scales = work3.tile([P, 2 * DM], U8, name="scales", align_bytes=64, bufs=4)
             w = 2 * DM if ok(k + 2) else DM
             nc.vector.quantize_mx(
                 out=codes[:, 0:w].bitcast(FP8X4), scales=scales[:, 0:w], in_=q_of(k)[:, 0 : 4 * w]
@@ -196,20 +197,26 @@ def tile_attractorstate_v2_t_kernel(tc, hidden_states, positional_encodings, W, 
         def st_RG(k):
             if not ok(k):
                 return
-            ggrp = work2.tile([P, 4 * DS], BF16, name="ggrp", align_bytes=64)
+            if k % 2 == 0:
+                ggrp_t[k // 2] = work2.tile([P, 8 * DS], BF16, name="ggrp", align_bytes=64)
+            half = ggrp_t[k // 2][:, (k % 2) * 4 * DS : (k % 2 + 1) * 4 * DS]
             nc.scalar.copy(
-                out=ggrp[:].bitcast(F32).rearrange("p (s a) -> p s a", a=2),
+                out=half.bitcast(F32).rearrange("p (s a) -> p s a", a=2),
                 in_=gps_t[k][:].rearrange("p a s -> p s a"),
             )
-            ggrp_t[k] = ggrp
 
-        def st_QG(k):
-            if not ok(k):
-                return
-            gcodes = work3.tile([P, DS], U32, name="gcodes", align_bytes=64)
-            gscales = work3.tile([P, DS], U8, name="gscales", align_bytes=64)
-            nc.vector.quantize_mx(out=gcodes[:].bitcast(FP8X4), scales=gscales[:], in_=ggrp_t[k][:])
-            gq_t[k] = (gcodes, gscales)
+        def st_QG(k, n):
+            w = n * DS
+            lo = (k % 2) * 4 * DS
+            gcodes = work3.tile([P, 2 * DS], U32, name="gcodes", align_bytes=64)
+            gscales = work3.tile([P, 2 * DS], U8, name="gscales", align_bytes=64)
+            nc.vector.quantize_mx(
+                out=gcodes[:, 0:w].bitcast(FP8X4),
+                scales=gscales[:, 0:w],
+                in_=ggrp_t[k // 2][:, lo : lo + 4 * w],
+            )
+            for i in range(n):
+                gq_t[k + i] = (gcodes[:, i * DS : (i + 1) * DS], gscales[:, i * DS : (i + 1) * DS])
 
         def st_RPs(k):
             if not ok(k):
@@ -222,15 +229,15 @@ def tile_attractorstate_v2_t_kernel(tc, hidden_states, positional_encodings, W, 
         def st_RPv(k):
             if not ok(k):
                 return
-            lo = (DM - G_COLS - V_COLS) // 4
-            hi = (DM - G_COLS) // 4
+            lo = S_COLS // 4
+            hi = (DM - G_COLS) // 4 if k >= G_FROM else DM // 4
             nc.vector.tensor_copy(
                 out=pgrp_of(k).rearrange("p (c i t) -> p c t i", i=4, t=4)[:, lo:hi],
                 in_=pe_t[k][:].rearrange("p (t c i) -> p c t i", t=4, i=4)[:, lo:hi],
             )
 
         def st_RPg(k):
-            if not ok(k):
+            if not ok(k) or k < G_FROM:
                 return
             lo = (DM - G_COLS) // 4
             nc.gpsimd.tensor_scalar(
@@ -287,10 +294,13 @@ def tile_attractorstate_v2_t_kernel(tc, hidden_states, positional_encodings, W, 
         nc.vector.memset(brow[:], 0.0)
         nc.sync.dma_start(out=brow[0:1, :], in_=b.unsqueeze(0))
         load_hs(1)
+        load_hs(2)
+        load_hs(3)
         load_pe(0)
-        for k in range(2, LOAD_AHEAD):
+        load_pe(1)
+        for k in range(4, LOAD_AHEAD):
             load_hs(k)
-            load_pe(k - 1)
+            load_pe(k - 2)
         ones = const.tile([P, 32], BF16, name="ones")
         nc.vector.memset(ones[:], 1.0)
 
@@ -302,12 +312,16 @@ def tile_attractorstate_v2_t_kernel(tc, hidden_states, positional_encodings, W, 
         nc.vector.tensor_copy(out=age_f[:], in_=age_i[:])
         wtab = const.tile([P, SEQ], F32, name="wtab")
         nc.scalar.activation(out=wtab[:, SEQ - CHUNK : SEQ], in_=age_f[:], func=ACT.Exp, scale=-step)
-        for c in range(CPB - 1):
-            nc.vector.tensor_scalar_mul(
-                out=wtab[:, c * CHUNK : (c + 1) * CHUNK],
-                in0=wtab[:, SEQ - CHUNK : SEQ],
-                scalar1=math.exp(-step * CHUNK * (CPB - 1 - c)),
-            )
+
+        def decay(lo, hi):
+            for c in range(lo, hi):
+                nc.vector.tensor_scalar_mul(
+                    out=wtab[:, c * CHUNK : (c + 1) * CHUNK],
+                    in0=wtab[:, SEQ - CHUNK : SEQ],
+                    scalar1=math.exp(-step * CHUNK * (CPB - 1 - c)),
+                )
+
+        decay(0, 4)
 
         w32 = w_sb[:].bitcast(F32)
         wt = psum.tile([P, 2, DS], F32, name="wt", tag="xt", bufs=2)
@@ -325,42 +339,59 @@ def tile_attractorstate_v2_t_kernel(tc, hidden_states, positional_encodings, W, 
         )
         wcodes = const.tile([P, DS], U32, name="wcodes", align_bytes=64)
         wscales = const.tile([P, DS], U8, name="wscales", align_bytes=64)
+        nc.vector.quantize_mx(out=wcodes[:].bitcast(FP8X4), scales=wscales[:], in_=wgrp[:])
+        decay(4, CPB - 1)
         st_T(0)
+        st_A(0)
+        st_T(1)
         bps = psum.tile([P, 2, 32], F32, name="bps", tag="gps")
         for h in range(2):
             nc.tensor.matmul(
                 out=bps[:, h, :], lhsT=brow[:, h * P : (h + 1) * P], rhs=ones[:], start=True, stop=True
             )
-        nc.vector.quantize_mx(out=wcodes[:].bitcast(FP8X4), scales=wscales[:], in_=wgrp[:])
+        st_QH(0)
         bcol = const.tile([P, 2], F32, name="bcol")
         nc.vector.tensor_copy(out=bcol[:], in_=bps[:, :, 0])
-        st_A(0)
-        st_T(1)
-        st_QH(0)
-        st_M1(0)
         st_A(1)
         st_T(2)
+        st_M1(0)
         st_QH(1)
-        for k in range(Q_BUFS):
-            st_RPg(k)
         st_A(2)
         st_RPs(0)
+        st_E(0)
         st_RPv(0)
-        st_RPs(1)
+        st_T(3)
+        st_M1(1)
+        st_A(3)
 
         for k in range(NCH + 2):
             load_hs(k + LOAD_AHEAD)
-            load_pe(k + LOAD_AHEAD - 1)
-            st_E(k)
-            st_M1(k + 1)
-            st_OUT(k - 2)
-            st_QG(k - 1)
+            load_pe(k + LOAD_AHEAD - 2)
+            if k > 0:
+                st_E(k)
+                st_M1(k + 1)
+            if k % 2 == 0:
+                st_OUT(k - 3)
+            if k % 2 == 0 and 2 <= k < NCH:
+                st_QG(k - 2, 2)
+            if k >= NCH - 1 and k <= NCH:
+                st_QG(k - 1, 1)
             st_TG(k)
-            st_T(k + 3)
+            if k > 0:
+                st_T(k + 3)
             st_RG(k)
-            st_A(k + 3)
-            st_M2(k - 1)
+            if k == 0:
+                st_RPs(1)
+            else:
+                st_A(k + 3)
+            if k % 2 == 0 and 2 <= k < NCH:
+                st_M2(k - 2)
+                st_M2(k - 1)
+            if k >= NCH - 1 and k <= NCH:
+                st_M2(k - 1)
             st_RPv(k + 1)
             st_Q(k)
             st_RPs(k + 2)
             st_RPg(k + Q_BUFS)
+            if k == NCH + 1:
+                st_OUT(NCH - 1)

@@ -284,6 +284,15 @@ def tile_attractorstate_v2_t_kernel(tc, hidden_states, positional_encodings, W, 
                 r0 = i * DS + h * P
                 nc.sync.dma_start(out=out_flat[r0 : r0 + P, :], in_=o_sb[:])
 
+        zeros = const.tile([P, DM], BF16, name="zeros")
+        nc.vector.memset(zeros[:], 0.0)
+        idle = psum.tile([P, DM], F32, name="idle", tag="acc0")
+
+        def st_warm(n):
+            for i in range(n):
+                nc.tensor.matmul(out=idle[:], lhsT=zeros[:, 0:P], rhs=zeros[:], start=True, stop=True)
+
+        st_warm(6)
         w_sb = const.tile([P, 2 * DM], BF16, name="w_sb")
         nc.sync.dma_start(
             out=w_sb[:].rearrange("p (h d) -> p h d", h=2),
@@ -342,8 +351,10 @@ def tile_attractorstate_v2_t_kernel(tc, hidden_states, positional_encodings, W, 
         nc.vector.quantize_mx(out=wcodes[:].bitcast(FP8X4), scales=wscales[:], in_=wgrp[:])
         decay(4, CPB - 1)
         st_T(0)
+        st_warm(2)
         st_A(0)
         st_T(1)
+        st_warm(2)
         bps = psum.tile([P, 2, 32], F32, name="bps", tag="gps")
         for h in range(2):
             nc.tensor.matmul(
@@ -384,11 +395,7 @@ def tile_attractorstate_v2_t_kernel(tc, hidden_states, positional_encodings, W, 
                 st_RPs(1)
             else:
                 st_A(k + 3)
-            if k % 2 == 0 and 2 <= k < NCH:
-                st_M2(k - 2)
-                st_M2(k - 1)
-            if k >= NCH - 1 and k <= NCH:
-                st_M2(k - 1)
+            st_M2(k - 2)
             st_RPv(k + 1)
             st_Q(k)
             st_RPs(k + 2)

@@ -25,8 +25,8 @@ CPB = SEQ // CHUNK
 NCH = BATCH * CPB
 LOAD_AHEAD = 6
 S_COLS = 272
-V_COLS = 56
-G_COLS = 184
+V_COLS = 72
+G_COLS = 168
 Q_BUFS = 3
 G_FROM = 4
 
@@ -136,8 +136,8 @@ def tile_attractorstate_v2_t_kernel(tc, hidden_states, positional_encodings, W, 
         def st_Q(k):
             if not ok(k):
                 return
-            codes = work3.tile([P, 2 * DM], U32, name="codes", align_bytes=64, bufs=4)
-            scales = work3.tile([P, 2 * DM], U8, name="scales", align_bytes=64, bufs=4)
+            codes = work3.tile([P, 2 * DM], U32, name="codes", align_bytes=64)
+            scales = work3.tile([P, 2 * DM], U8, name="scales", align_bytes=64)
             w = 2 * DM if ok(k + 2) else DM
             nc.vector.quantize_mx(
                 out=codes[:, 0:w].bitcast(FP8X4), scales=scales[:, 0:w], in_=q_of(k)[:, 0 : 4 * w]
@@ -197,26 +197,24 @@ def tile_attractorstate_v2_t_kernel(tc, hidden_states, positional_encodings, W, 
         def st_RG(k):
             if not ok(k):
                 return
-            if k % 2 == 0:
-                ggrp_t[k // 2] = work2.tile([P, 8 * DS], BF16, name="ggrp", align_bytes=64)
-            half = ggrp_t[k // 2][:, (k % 2) * 4 * DS : (k % 2 + 1) * 4 * DS]
-            nc.scalar.copy(
-                out=half.bitcast(F32).rearrange("p (s a) -> p s a", a=2),
-                in_=gps_t[k][:].rearrange("p a s -> p s a"),
-            )
-
-        def st_QG(k, n):
-            w = n * DS
-            lo = (k % 2) * 4 * DS
-            gcodes = work3.tile([P, 2 * DS], U32, name="gcodes", align_bytes=64)
-            gscales = work3.tile([P, 2 * DS], U8, name="gscales", align_bytes=64)
-            nc.vector.quantize_mx(
-                out=gcodes[:, 0:w].bitcast(FP8X4),
-                scales=gscales[:, 0:w],
-                in_=ggrp_t[k // 2][:, lo : lo + 4 * w],
-            )
+            ggrp = work2.tile([P, 4 * DS], BF16, name="ggrp", align_bytes=64)
+            g32 = ggrp[:].bitcast(F32).rearrange("p (s a) -> p s a", a=2)
+            n = 2 if k == NCH - 1 else 1
+            w = DS // n
             for i in range(n):
-                gq_t[k + i] = (gcodes[:, i * DS : (i + 1) * DS], gscales[:, i * DS : (i + 1) * DS])
+                nc.scalar.copy(
+                    out=g32[:, i * w : (i + 1) * w, :],
+                    in_=gps_t[k][:, :, i * w : (i + 1) * w].rearrange("p a s -> p s a"),
+                )
+            ggrp_t[k] = ggrp
+
+        def st_QG(k):
+            if not ok(k):
+                return
+            gcodes = work3.tile([P, DS], U32, name="gcodes", align_bytes=64)
+            gscales = work3.tile([P, DS], U8, name="gscales", align_bytes=64)
+            nc.vector.quantize_mx(out=gcodes[:].bitcast(FP8X4), scales=gscales[:], in_=ggrp_t[k][:])
+            gq_t[k] = (gcodes, gscales)
 
         def st_RPs(k):
             if not ok(k):
@@ -275,14 +273,18 @@ def tile_attractorstate_v2_t_kernel(tc, hidden_states, positional_encodings, W, 
             if not ok(k) or k % CPB != CPB - 1:
                 return
             i = k // CPB
-            for h in range(2):
-                o_sb = work2.tile([P, DM], F32, name="o_sb%d" % h)
-                if h == 0:
-                    nc.vector.tensor_copy(out=o_sb[:], in_=acc_t[i][h][:])
-                else:
-                    nc.scalar.copy(out=o_sb[:], in_=acc_t[i][h][:])
-                r0 = i * DS + h * P
-                nc.sync.dma_start(out=out_flat[r0 : r0 + P, :], in_=o_sb[:])
+            n = 2 if k == NCH - 1 else 1
+            w = DM // n
+            for part in range(n):
+                for h in range(2):
+                    o_sb = work2.tile([P, w], F32, name="o_sb%d" % h)
+                    src = acc_t[i][h][:, part * w : (part + 1) * w]
+                    if h == 0:
+                        nc.vector.tensor_copy(out=o_sb[:], in_=src)
+                    else:
+                        nc.scalar.copy(out=o_sb[:], in_=src)
+                    r0 = i * DS + h * P
+                    nc.sync.dma_start(out=out_flat[r0 : r0 + P, part * w : (part + 1) * w], in_=o_sb[:])
 
         zeros = const.tile([P, DM], BF16, name="zeros")
         nc.vector.memset(zeros[:], 0.0)
@@ -333,7 +335,7 @@ def tile_attractorstate_v2_t_kernel(tc, hidden_states, positional_encodings, W, 
         decay(0, 4)
 
         w32 = w_sb[:].bitcast(F32)
-        wt = psum.tile([P, 2, DS], F32, name="wt", tag="xt", bufs=2)
+        wt = psum.tile([P, 2, DS], F32, name="wt", tag="hp", bufs=3)
         for h in range(2):
             for u in range(2):
                 nc.tensor.transpose(
@@ -381,12 +383,8 @@ def tile_attractorstate_v2_t_kernel(tc, hidden_states, positional_encodings, W, 
             if k > 0:
                 st_E(k)
                 st_M1(k + 1)
-            if k % 2 == 0:
-                st_OUT(k - 3)
-            if k % 2 == 0 and 2 <= k < NCH:
-                st_QG(k - 2, 2)
-            if k >= NCH - 1 and k <= NCH:
-                st_QG(k - 1, 1)
+            st_OUT(k - 2)
+            st_QG(k - 1)
             st_TG(k)
             if k > 0:
                 st_T(k + 3)
@@ -395,10 +393,8 @@ def tile_attractorstate_v2_t_kernel(tc, hidden_states, positional_encodings, W, 
                 st_RPs(1)
             else:
                 st_A(k + 3)
-            st_M2(k - 2)
+            st_M2(k - 1)
             st_RPv(k + 1)
             st_Q(k)
             st_RPs(k + 2)
             st_RPg(k + Q_BUFS)
-            if k == NCH + 1:
-                st_OUT(NCH - 1)

@@ -24,10 +24,10 @@ CHUNK = 512
 CPB = SEQ // CHUNK
 NCH = BATCH * CPB
 LOAD_AHEAD = 6
-S_COLS = 272
-V_COLS = 72
-G_COLS = 168
-Q_BUFS = 3
+S_COLS = 264
+V_COLS = 64
+G_COLS = 184
+Q_BUFS = 4
 G_FROM = 4
 
 
@@ -136,8 +136,8 @@ def tile_attractorstate_v2_t_kernel(tc, hidden_states, positional_encodings, W, 
         def st_Q(k):
             if not ok(k):
                 return
-            codes = work3.tile([P, 2 * DM], U32, name="codes", align_bytes=64)
-            scales = work3.tile([P, 2 * DM], U8, name="scales", align_bytes=64)
+            codes = work3.tile([P, 2 * DM], U32, name="codes", align_bytes=64, bufs=4)
+            scales = work3.tile([P, 2 * DM], U8, name="scales", align_bytes=64, bufs=4)
             w = 2 * DM if ok(k + 2) else DM
             nc.vector.quantize_mx(
                 out=codes[:, 0:w].bitcast(FP8X4), scales=scales[:, 0:w], in_=q_of(k)[:, 0 : 4 * w]
@@ -377,14 +377,13 @@ def tile_attractorstate_v2_t_kernel(tc, hidden_states, positional_encodings, W, 
         st_M1(1)
         st_A(3)
 
-        for k in range(NCH + 2):
+        for k in range(NCH + 3):
             load_hs(k + LOAD_AHEAD)
             load_pe(k + LOAD_AHEAD - 2)
             if k > 0:
                 st_E(k)
                 st_M1(k + 1)
-            st_OUT(k - 2)
-            st_QG(k - 1)
+            st_OUT(k - 3)
             st_TG(k)
             if k > 0:
                 st_T(k + 3)
@@ -393,8 +392,9 @@ def tile_attractorstate_v2_t_kernel(tc, hidden_states, positional_encodings, W, 
                 st_RPs(1)
             else:
                 st_A(k + 3)
-            st_M2(k - 1)
+            st_M2(k - 2)
             st_RPv(k + 1)
             st_Q(k)
+            st_QG(k - 1)
             st_RPs(k + 2)
             st_RPg(k + Q_BUFS)

import math
from contextlib import ExitStack

import concourse.mybir as mybir
from concourse.masks import make_identity

FLOPS = 2 * 4 * 4096 * 512 * 256 * 2

BF16 = mybir.dt.bfloat16
F32 = mybir.dt.float32
I32 = mybir.dt.int32
U32 = mybir.dt.uint32
U8 = mybir.dt.uint8
FP8X4 = mybir.dt.float8_e4m3fn_x4
ALU = mybir.AluOpType
ACT = mybir.ActivationFunctionType

P = 128
BATCH = 4
SEQ = 4096
DM = 512
DS = 256
CHUNK = 512
CPB = SEQ // CHUNK
NCH = BATCH * CPB
LOAD_AHEAD = 6
S_COLS = 264
V_COLS = 64
G_COLS = 184
Q_BUFS = 4
G_FROM = 4


def tile_attractorstate_v2_t_kernel(tc, hidden_states, positional_encodings, W, b, out):
    nc = tc.nc
    hs_flat = hidden_states.flatten_outer_dims()
    pe_flat = positional_encodings.flatten_outer_dims()
    out_flat = out.flatten_outer_dims()
    step = math.pi / SEQ

    with ExitStack() as ctx:
        ctx.enter_context(tc.manual_schedule())
        const = ctx.enter_context(tc.tile_pool(name="const", bufs=1))
        loads = ctx.enter_context(tc.tile_pool(name="loads", bufs=LOAD_AHEAD + 2))
        work2 = ctx.enter_context(tc.tile_pool(name="work2", bufs=2))
        work3 = ctx.enter_context(tc.tile_pool(name="work3", bufs=3))
        psum = ctx.enter_context(tc.psum_pool(name="psum", bufs=1))

        hs_t = {}
        pe_t = {}
        xt_t = {}
        h_in = {}
        hq_t = {}
        hp_t = {}
        gt_t = {}
        gps_t = {}
        ggrp_t = {}
        gq_t = {}
        q_in = {}
        pq_t = {}
        acc_t = {}
        pi_t = {}

        def ok(k):
            return 0 <= k < NCH

        def load_hs(k, parts=1):
            if not ok(k):
                return
            hs_sb = loads.tile([P, 4 * DM], BF16, name="hs_sb")
            view = hs_flat[k * CHUNK : (k + 1) * CHUNK, :].rearrange("(p j) d -> p (j d)", j=4)
            w = 4 * DM // parts
            for i in range(parts):
                nc.sync.dma_start(out=hs_sb[:, i * w : (i + 1) * w], in_=view[:, i * w : (i + 1) * w])
            hs_t[k] = hs_sb

        def load_pe(k):
            if not ok(k):
                return
            pe_sb = loads.tile([P, 4 * DM], BF16, name="pe_sb")
            nc.sync.dma_start(
                out=pe_sb[:],
                in_=pe_flat[k * CHUNK : (k + 1) * CHUNK, :].rearrange("(p j) d -> p (j d)", j=4),
            )
            pe_t[k] = pe_sb

        def q_of(k):
            if k not in q_in:
                q_in[k] = work3.tile([P, 8 * DM], BF16, name="q_in", align_bytes=64, bufs=Q_BUFS)
            return q_in[k]

        def pgrp_of(k):
            return q_of(k)[:, 0 : 4 * DM]

        def hgrp_of(k):
            if k >= 2:
                return q_of(k - 2)[:, 4 * DM : 8 * DM]
            if k not in h_in:
                h_in[k] = const.tile([P, 4 * CHUNK], BF16, name="h_in%d" % k, align_bytes=64)
            return h_in[k][:]

        def st_T(k):
            if not ok(k):
                return
            hs32 = hs_t[k][:].bitcast(F32)
            banks = []
            for a in range(2):
                xt = psum.tile([P, 2, 2, P], F32, name="xt", tag="xt", bufs=2)
                for jj in range(2):
                    j = 2 * a + jj
                    for u in range(2):
                        nc.tensor.transpose(
                            xt[:, jj, u, :],
                            hs32[:, j * 256 + u * P : j * 256 + (u + 1) * P],
                            ident[:],
                        )
                banks.append(xt)
            xt_t[k] = banks

        def st_A(k):
            if not ok(k):
                return
            h32 = hgrp_of(k).bitcast(F32).rearrange("q (a t j u) -> q a t j u", a=2, j=2, u=2)
            for a in range(2):
                nc.scalar.copy(
                    out=h32[:, a, :, :, :],
                    in_=xt_t[k][a][:].rearrange("q j u t -> q t j u"),
                )

        def st_QH(k):
            hcodes = const.tile([P, CHUNK], U32, name="hcodes%d" % k, align_bytes=64)
            hscales = const.tile([P, CHUNK], U8, name="hscales%d" % k, align_bytes=64)
            nc.vector.quantize_mx(out=hcodes[:].bitcast(FP8X4), scales=hscales[:], in_=hgrp_of(k))
            hq_t[k] = (hcodes[:], hscales[:])

        def st_Q(k):
            if not ok(k):
                return
            codes = work3.tile([P, 2 * DM], U32, name="codes", align_bytes=64, bufs=4)
            scales = work3.tile([P, 2 * DM], U8, name="scales", align_bytes=64, bufs=4)
            w = 2 * DM if ok(k + 2) else DM
            nc.vector.quantize_mx(
                out=codes[:, 0:w].bitcast(FP8X4), scales=scales[:, 0:w], in_=q_of(k)[:, 0 : 4 * w]
            )
            pq_t[k] = (codes[:, 0:DM], scales[:, 0:DM])
            hq_t[k + 2] = (codes[:, DM : 2 * DM], scales[:, DM : 2 * DM])

        def st_M1(k):
            if not ok(k):
                return
            hcodes, hscales = hq_t[k]
            banks = []
            for h in range(2):
                hp = psum.tile([P, CHUNK], F32, name="hp", tag="hp", bufs=3)
                nc.tensor.matmul_mx(
                    out=hp[:],
                    lhsT=wcodes[:, h * P : (h + 1) * P].bitcast(FP8X4),
                    lhsT_scale=wscales[:, h * P : (h + 1) * P],
                    rhs=hcodes.bitcast(FP8X4),
                    rhs_scale=hscales,
                    start=True,
                    stop=True,
                )
                banks.append(hp)
            hp_t[k] = banks

        def st_E(k):
            if not ok(k):
                return
            c = k % CPB
            gt = work2.tile([P, 2, CHUNK], BF16, name="gt")
            for h in range(2):
                nc.vector.scalar_tensor_tensor(
                    out=gt[:, h, :],
                    in0=hp_t[k][h][:],
                    scalar=bcol[:, h : h + 1],
                    in1=wtab[:, c * CHUNK : (c + 1) * CHUNK],
                    op0=ALU.add,
                    op1=ALU.mult,
                )
            gt_t[k] = gt

        def st_TG(k):
            if not ok(k):
                return
            g32 = gt_t[k][:].rearrange("s h n -> s (h n)").bitcast(F32)
            gps = psum.tile([P, 2, DS], F32, name="gps", tag="gps")
            for h in range(2):
                for a in range(2):
                    nc.tensor.transpose(
                        gps[:, a, h * P : (h + 1) * P],
                        g32[:, h * 256 + a * P : h * 256 + (a + 1) * P],
                        ident[:],
                    )
            gps_t[k] = gps

        def st_RG(k):
            if not ok(k):
                return
            ggrp = work2.tile([P, 4 * DS], BF16, name="ggrp", align_bytes=64)
            g32 = ggrp[:].bitcast(F32).rearrange("p (s a) -> p s a", a=2)
            n = 2 if k == NCH - 1 else 1
            w = DS // n
            for i in range(n):
                nc.scalar.copy(
                    out=g32[:, i * w : (i + 1) * w, :],
                    in_=gps_t[k][:, :, i * w : (i + 1) * w].rearrange("p a s -> p s a"),
                )
            ggrp_t[k] = ggrp

        def st_QG(k):
            if not ok(k):
                return
            gcodes = work3.tile([P, DS], U32, name="gcodes", align_bytes=64)
            gscales = work3.tile([P, DS], U8, name="gscales", align_bytes=64)
            nc.vector.quantize_mx(out=gcodes[:].bitcast(FP8X4), scales=gscales[:], in_=ggrp_t[k][:])
            gq_t[k] = (gcodes, gscales)

        def st_RPs(k):
            if not ok(k):
                return
            nc.scalar.copy(
                out=pgrp_of(k).rearrange("p (c i t) -> p c t i", i=4, t=4)[:, 0 : S_COLS // 4],
                in_=pe_t[k][:].rearrange("p (t c i) -> p c t i", t=4, i=4)[:, 0 : S_COLS // 4],
            )

        def st_RPv(k):
            if not ok(k):
                return
            lo = S_COLS // 4
            hi = (DM - G_COLS) // 4 if k >= G_FROM else DM // 4
            nc.vector.tensor_copy(
                out=pgrp_of(k).rearrange("p (c i t) -> p c t i", i=4, t=4)[:, lo:hi],
                in_=pe_t[k][:].rearrange("p (t c i) -> p c t i", t=4, i=4)[:, lo:hi],
            )

        def st_RPg(k):
            if not ok(k) or k < G_FROM:
                return
            lo = (DM - G_COLS) // 4
            nc.gpsimd.tensor_scalar(
                out=pgrp_of(k).rearrange("p (c i t) -> p c t i", i=4, t=4)[:, lo:],
                in0=pe_t[k][:].rearrange("p (t c i) -> p c t i", t=4, i=4)[:, lo:],
                scalar1=1.0,
                scalar2=0.0,
                op0=ALU.mult,
                op1=ALU.add,
            )

        def st_M2(k):
            if not ok(k):
                return
            i = k // CPB
            c = k % CPB
            if c == 0:
                acc0 = psum.tile([P, DM], F32, name="acc0", tag="acc0")
                acc1 = psum.tile([P, DM], F32, name="acc1", tag="acc1")
                acc_t[i] = (acc0, acc1)
            gcodes, gscales = gq_t[k]
            pcodes, pscales = pq_t[k]
            for h in range(2):
                nc.tensor.matmul_mx(
                    out=acc_t[i][h][:],
                    lhsT=gcodes[:, h * P : (h + 1) * P].bitcast(FP8X4),
                    lhsT_scale=gscales[:, h * P : (h + 1) * P],
                    rhs=pcodes.bitcast(FP8X4),
                    rhs_scale=pscales,
                    start=(c == 0),
                    stop=(c == CPB - 1),
                )

        def st_OUT(k):
            if not ok(k) or k % CPB != CPB - 1:
                return
            i = k // CPB
            n = 2 if k == NCH - 1 else 1
            w = DM // n
            for part in range(n):
                for h in range(2):
                    o_sb = work2.tile([P, w], F32, name="o_sb%d" % h)
                    src = acc_t[i][h][:, part * w : (part + 1) * w]
                    if h == 0:
                        nc.vector.tensor_copy(out=o_sb[:], in_=src)
                    else:
                        nc.scalar.copy(out=o_sb[:], in_=src)
                    r0 = i * DS + h * P
                    nc.sync.dma_start(out=out_flat[r0 : r0 + P, part * w : (part + 1) * w], in_=o_sb[:])

        zeros = const.tile([P, DM], BF16, name="zeros")
        nc.vector.memset(zeros[:], 0.0)
        idle = psum.tile([P, DM], F32, name="idle", tag="acc0")

        def st_warm(n):
            for i in range(n):
                nc.tensor.matmul(out=idle[:], lhsT=zeros[:, 0:P], rhs=zeros[:], start=True, stop=True)

        st_warm(6)
        w_sb = const.tile([P, 2 * DM], BF16, name="w_sb")
        nc.sync.dma_start(
            out=w_sb[:].rearrange("p (h d) -> p h d", h=2),
            in_=W.rearrange("(h p) d -> p h d", p=P),
        )
        load_hs(0, parts=2)
        brow = const.tile([P, DS], BF16, name="brow")
        nc.vector.memset(brow[:], 0.0)
        nc.sync.dma_start(out=brow[0:1, :], in_=b.unsqueeze(0))
        load_hs(1)
        load_hs(2)
        load_hs(3)
        load_pe(0)
        load_pe(1)
        for k in range(4, LOAD_AHEAD):
            load_hs(k)
            load_pe(k - 2)
        ones = const.tile([P, 32], BF16, name="ones")
        nc.vector.memset(ones[:], 1.0)

        age_i = const.tile([P, CHUNK], I32, name="age_i")
        nc.gpsimd.iota(age_i[:], pattern=[[-2, 2], [-4, P], [-1, 2]], base=CHUNK - 1, channel_multiplier=0)
        ident = const.tile([P, P], F32, name="ident")
        make_identity(nc, ident[:])
        age_f = const.tile([P, CHUNK], F32, name="age_f")
        nc.vector.tensor_copy(out=age_f[:], in_=age_i[:])
        wtab = const.tile([P, SEQ], F32, name="wtab")
        nc.scalar.activation(out=wtab[:, SEQ - CHUNK : SEQ], in_=age_f[:], func=ACT.Exp, scale=-step)

        def decay(lo, hi):
            for c in range(lo, hi):
                nc.vector.tensor_scalar_mul(
                    out=wtab[:, c * CHUNK : (c + 1) * CHUNK],
                    in0=wtab[:, SEQ - CHUNK : SEQ],
                    scalar1=math.exp(-step * CHUNK * (CPB - 1 - c)),
                )

        decay(0, 4)

        w32 = w_sb[:].bitcast(F32)
        wt = psum.tile([P, 2, DS], F32, name="wt", tag="hp", bufs=3)
        for h in range(2):
            for u in range(2):
                nc.tensor.transpose(
                    wt[:, u, h * P : (h + 1) * P],
                    w32[:, h * 256 + u * P : h * 256 + (u + 1) * P],
                    ident[:],
                )
        wgrp = const.tile([P, 4 * DS], BF16, name="wgrp", align_bytes=64)
        nc.vector.tensor_copy(
            out=wgrp[:].bitcast(F32).rearrange("q (s u) -> q s u", u=2),
            in_=wt[:].rearrange("q u s -> q s u"),
        )
        wcodes = const.tile([P, DS], U32, name="wcodes", align_bytes=64)
        wscales = const.tile([P, DS], U8, name="wscales", align_bytes=64)
        nc.vector.quantize_mx(out=wcodes[:].bitcast(FP8X4), scales=wscales[:], in_=wgrp[:])
        decay(4, CPB - 1)
        st_T(0)
        st_warm(2)
        st_A(0)
        st_T(1)
        st_warm(2)
        bps = psum.tile([P, 2, 32], F32, name="bps", tag="gps")
        for h in range(2):
            nc.tensor.matmul(
                out=bps[:, h, :], lhsT=brow[:, h * P : (h + 1) * P], rhs=ones[:], start=True, stop=True
            )
        st_QH(0)
        bcol = const.tile([P, 2], F32, name="bcol")
        nc.vector.tensor_copy(out=bcol[:], in_=bps[:, :, 0])
        st_A(1)
        st_T(2)
        st_M1(0)
        st_QH(1)
        st_A(2)
        st_RPs(0)
        st_E(0)
        st_RPv(0)
        st_T(3)
        st_M1(1)
        st_A(3)

        for k in range(NCH + 3):
            load_hs(k + LOAD_AHEAD)
            load_pe(k + LOAD_AHEAD - 2)
            if k > 0:
                st_E(k)
                st_M1(k + 1)
            st_OUT(k - 3)
            st_TG(k)
            if k > 0:
                st_T(k + 3)
            st_RG(k)
            if k == 0:
                st_RPs(1)
            else:
                st_A(k + 3)
            st_M2(k - 2)
            st_RPv(k + 1)
            st_Q(k)
            st_QG(k - 1)
            st_RPs(k + 2)
            st_RPg(k + Q_BUFS)
